import numpy as np
import ml_dtypes

BF16 = ml_dtypes.bfloat16


def bf(x):
    return np.asarray(x, np.float32).astype(BF16)


def f32(x):
    return np.asarray(x, np.float32)


def f64(x):
    return np.asarray(x).astype(np.float64)


def striped(idx):
    return np.tile(idx.reshape(-1, 16).T, (8, 1))


B, A, C, S, K, E, N = 4, 64, 512, 4096, 128, 3, 256
VMAX = 8.0
EPS = 1e-6
BOX = 5.0


def softplus(v):
    return np.log(1.0 + np.exp(v))


def silu(v):
    return v / (1.0 + np.exp(-v))


def setup_inputs():
    return {
        "table": f32(0.3 * np.random.standard_normal((C, S))),
        "cart": f32(BOX * np.random.random((E, N))),
        "edge_w0": bf(np.random.standard_normal((K, C))),
        "edge_b0": f32(0.1 * np.random.standard_normal((C, 1))),
        "node_w0": bf(0.2 * np.random.standard_normal((C, C)) / np.sqrt(C)),
        "node_b0": f32(0.1 * np.random.standard_normal((C, 1))),
        "edge_w1": bf(np.random.standard_normal((K, C))),
        "edge_b1": f32(0.1 * np.random.standard_normal((C, 1))),
        "node_w1": bf(0.25 * np.random.standard_normal((C, C)) / np.sqrt(C)),
        "node_b1": f32(0.1 * np.random.standard_normal((C, 1))),
        "offs": striped(np.random.permutation(np.tile(np.arange(S), 2))[:N]),
    }


def reference(table, cart, edge_w0, edge_b0, node_w0, node_b0, edge_w1, edge_b1, node_w1, node_b1, offs):
    idx = offs[:16].T.reshape(-1)
    h = f64(table)[:, idx].reshape(C, B, A)
    x = f64(cart).reshape(E, B, A)
    diff = x[:, :, :, None] - x[:, :, None, :]
    d = np.sqrt((diff * diff).sum(axis=0) + EPS)
    centers = np.linspace(0.0, VMAX, K)
    gamma = 1.0 / (VMAX / K) ** 2
    rbf = np.exp(-gamma * (d[None] - centers[:, None, None, None]) ** 2).reshape(K, B * A * A)
    layers = ((edge_w0, edge_b0, node_w0, node_b0), (edge_w1, edge_b1, node_w1, node_b1))
    for ew, eb, nw, nb in layers:
        gate = softplus(f64(ew).T @ rbf + f64(eb)).reshape(C, B, A, A)
        agg = (h[:, :, None, :] * gate).sum(axis=3).reshape(C, N)
        z = f64(nw).T @ agg + f64(nb)
        h = h + silu(z).reshape(C, B, A)
    return h.reshape(C, N)

@@ -1,0 +1,212 @@
+import concourse.mybir as mybir
+from concourse.masks import make_identity
+
+F32 = mybir.dt.float32
+BF16 = mybir.dt.bfloat16
+I32 = mybir.dt.int32
+U16 = mybir.dt.uint16
+ACT = mybir.ActivationFunctionType
+ALU = mybir.AluOpType
+AXIS = mybir.AxisListType
+
+P = 128
+C = 512
+CB = C // P
+S = 4096
+K = 128
+N = 256
+A = 64
+Q = N // A
+XYZ = 3
+PAIRS = A * N
+BANK = 512
+CHUNKS = PAIRS // BANK
+VMAX = 8.0
+GAMMA = 1.0 / (VMAX / K) ** 2
+EPS = 1e-6
+HALF = PAIRS // 2
+ROWS = 8
+
+FLOPS = 2 * (2 * K * C * PAIRS + 2 * C * C * N)
+
+
+def tile_crystalencoder_b_kernel(
+    tc, table, cart, edge_w0, edge_b0, node_w0, node_b0, edge_w1, edge_b1, node_w1, node_b1, offs, out
+):
+    nc = tc.nc
+    with tc.tile_pool(name="held", bufs=1) as held:
+        offsets = held.tile([P, N // 16], U16, name="offsets")
+        nc.sync.dma_start(offsets[:], offs)
+
+        edge_w = [held.tile([K, C], BF16, name=f"edge_w{l}") for l in range(2)]
+        node_w = [held.tile([P, CB, C], BF16, name=f"node_w{l}") for l in range(2)]
+        edge_b = [held.tile([P, CB], F32, name=f"edge_b{l}") for l in range(2)]
+        node_b = [held.tile([P, CB], F32, name=f"node_b{l}") for l in range(2)]
+        tables = [held.tile([P, S], F32, name=f"table{cb}") for cb in range(CB)]
+        rbf = held.tile([K, PAIRS], BF16, name="rbf")
+        h1 = [held.tile([P, N], F32, name=f"h1_{cb}") for cb in range(CB)]
+        one = held.tile([P, 1], F32, name="one")
+        nc.vector.memset(one[:], 1.0)
+
+        with (
+            tc.tile_pool(name="geometry", bufs=1) as geometry,
+            tc.tile_pool(name="squares", bufs=2) as squares,
+            tc.psum_pool(name="spread", bufs=2) as spread,
+        ):
+            atoms = geometry.tile([CHUNKS, XYZ * N], F32, name="atoms")
+            nc.sync.dma_start(atoms[:], cart.rearrange("e t -> (e t)").partition_broadcast(CHUNKS))
+            partners = geometry.tile([CHUNKS, XYZ * Q, 2], F32, name="partners")
+            nc.sync.dma_start(partners[:], cart.rearrange("e (q i a) -> i (e q) a", q=Q, i=CHUNKS, a=2))
+
+            for l, (w, b, nw, nb) in enumerate(
+                ((edge_w0, edge_b0, node_w0, node_b0), (edge_w1, edge_b1, node_w1, node_b1))
+            ):
+                nc.scalar.dma_start(edge_w[l][:], w)
+                nc.scalar.dma_start(node_w[l][:], nw.rearrange("(m p) c -> p m c", p=P))
+                with nc.allow_non_contiguous_dma(reason="one bias value to a partition"):
+                    nc.scalar.dma_start(edge_b[l][:], b.rearrange("(a p) o -> p (a o)", p=P))
+                    nc.scalar.dma_start(node_b[l][:], nb.rearrange("(a p) o -> p (a o)", p=P))
+            for cb in range(CB):
+                queue = nc.sync if cb % 2 == 0 else nc.gpsimd
+                queue.dma_start(tables[cb][:], table[cb * P : (cb + 1) * P, :])
+
+            identity = geometry.tile([P, P], F32, name="identity")
+            make_identity(nc, identity[:])
+            pick = geometry.tile([P, CHUNKS, P], F32, name="pick")
+            nc.vector.tensor_copy(pick[:], identity[:, 0:CHUNKS].unsqueeze(2).to_broadcast([P, CHUNKS, P]))
+            basis_index = geometry.tile([K, 1], I32, name="basis_index")
+            nc.gpsimd.iota(basis_index[:], pattern=[[0, 1]], base=0, channel_multiplier=1)
+            minus_center = geometry.tile([K, 1], F32, name="minus_center")
+            nc.vector.tensor_scalar_mul(minus_center[:], basis_index[:], -VMAX / (K - 1))
+
+            diff = geometry.tile([CHUNKS, 2, XYZ * Q, A], F32, name="diff")
+            for a in range(2):
+                nc.vector.tensor_tensor(
+                    diff[:, a],
+                    atoms[:].rearrange("p (g j) -> p g j", j=A),
+                    partners[:, :, a : a + 1].to_broadcast([CHUNKS, XYZ * Q, A]),
+                    ALU.subtract,
+                )
+            nc.vector.tensor_tensor(diff[:], diff[:], diff[:], ALU.mult)
+            square = diff[:].rearrange("p a (e q) j -> p a e (q j)", e=XYZ)
+            dist = geometry.tile([P, 2, N], F32, name="dist")
+            nc.vector.memset(dist[:], 0.0)
+            nc.vector.tensor_tensor(dist[0:CHUNKS], square[:, :, 0], square[:, :, 1], ALU.add)
+            nc.vector.scalar_tensor_tensor(
+                dist[0:CHUNKS], dist[0:CHUNKS], EPS, square[:, :, 2], op0=ALU.add, op1=ALU.add
+            )
+            nc.scalar.activation(dist[0:CHUNKS], dist[0:CHUNKS], ACT.Sqrt)
+
+            for g in range(CHUNKS // 4):
+                gap2 = squares.tile([K, 4 * BANK], F32, name="gap2")
+                for u in range(4):
+                    d_everywhere = spread.tile([K, BANK], F32, name="d_everywhere")
+                    nc.tensor.matmul(
+                        d_everywhere[:],
+                        pick[:, 4 * g + u, :],
+                        dist[:].rearrange("p a t -> p (a t)"),
+                        start=True,
+                        stop=True,
+                    )
+                    nc.scalar.activation(
+                        gap2[:, u * BANK : (u + 1) * BANK], d_everywhere[:], ACT.Square, bias=minus_center[:]
+                    )
+                nc.scalar.activation(rbf[:, g * 4 * BANK : (g + 1) * 4 * BANK], gap2[:], ACT.Exp, scale=-GAMMA)
+
+        with (
+            tc.tile_pool(name="gates", bufs=2) as gates,
+            tc.tile_pool(name="products", bufs=2) as products,
+            tc.tile_pool(name="small", bufs=2) as small,
+            tc.psum_pool(name="banks", bufs=6) as banks,
+            tc.psum_pool(name="node", bufs=2) as node,
+        ):
+
+            def make_gates(l, cb, half):
+                gate = gates.tile([P, HALF], F32, name="gate")
+                for u in range(HALF // BANK):
+                    first = half * HALF + u * BANK
+                    pre = banks.tile([P, BANK], F32, name="pre")
+                    nc.tensor.matmul(
+                        pre[:], edge_w[l][:, cb * P : (cb + 1) * P], rbf[:, first : first + BANK], start=True, stop=True
+                    )
+                    nc.scalar.activation(
+                        gate[:, u * BANK : (u + 1) * BANK], pre[:], ACT.Exp, bias=edge_b[l][:, cb : cb + 1]
+                    )
+                for g in range(HALF // (ROWS * N)):
+                    rows = gate[:, g * ROWS * N : (g + 1) * ROWS * N]
+                    nc.scalar.activation(rows, rows, ACT.Ln, bias=one[:])
+                return gate
+
+            def sum_over_partners(sums, first_rho, product):
+                nc.vector.tensor_reduce(
+                    sums[:, first_rho : first_rho + ROWS, :],
+                    product[:].rearrange("p a (q j) -> p a q j", j=A),
+                    axis=AXIS.X,
+                    op=ALU.add,
+                )
+
+            def to_list_order(agg, cb, sums):
+                nc.vector.tensor_copy(
+                    agg[:, cb, :].rearrange("p (q r) -> p q r", q=Q), sums[:].rearrange("p r q -> p q r")
+                )
+
+            def node_update(l, agg, ob):
+                z = node.tile([P, N], F32, name="z")
+                for mb in range(CB):
+                    nc.tensor.matmul(
+                        z[:], node_w[l][:, mb, ob * P : (ob + 1) * P], agg[:, mb, :], start=(mb == 0), stop=(mb == CB - 1)
+                    )
+                step = small.tile([P, N], F32, name="step")
+                nc.scalar.activation(step[:], z[:], ACT.Silu, bias=node_b[l][:, ob : ob + 1])
+                return step
+
+            agg0 = held.tile([P, CB, N], BF16, name="agg0")
+            for cb in range(CB):
+                sums = small.tile([P, A, Q], F32, name="sums")
+                for half in range(2):
+                    gate = make_gates(0, cb, half)
+                    for g in range(HALF // (ROWS * N)):
+                        product = products.tile([P, ROWS, N], F32, name="product")
+                        for a in range(ROWS):
+                            row = g * ROWS + a
+                            nc.vector.tensor_tensor(
+                                product[:, a, :],
+                                tables[cb][:].indirect(offsets[:]),
+                                gate[:, row * N : (row + 1) * N],
+                                ALU.mult,
+                            )
+                        sum_over_partners(sums, half * (A // 2) + g * ROWS, product)
+                to_list_order(agg0, cb, sums)
+
+            for ob in range(CB):
+                step = node_update(0, agg0, ob)
+                for piece in range(2):
+                    entries = slice(piece * (N // 2), (piece + 1) * (N // 2))
+                    nc.vector.tensor_tensor(
+                        h1[ob][:, entries],
+                        tables[ob][:].indirect(offsets[:, piece * (N // 32) : (piece + 1) * (N // 32)]),
+                        step[:, entries],
+                        ALU.add,
+                    )
+
+            agg1 = held.tile([P, CB, N], BF16, name="agg1")
+            for cb in range(CB):
+                sums = small.tile([P, A, Q], F32, name="sums")
+                for half in range(2):
+                    gate = make_gates(1, cb, half)
+                    for g in range(HALF // (ROWS * N)):
+                        product = products.tile([P, ROWS, N], F32, name="product")
+                        nc.vector.tensor_tensor(
+                            product[:],
+                            gate[:, g * ROWS * N : (g + 1) * ROWS * N].rearrange("p (a t) -> p a t", t=N),
+                            h1[cb][:].unsqueeze(1).to_broadcast([P, ROWS, N]),
+                            ALU.mult,
+                        )
+                        sum_over_partners(sums, half * (A // 2) + g * ROWS, product)
+                to_list_order(agg1, cb, sums)
+
+            for ob in range(CB):
+                step = node_update(1, agg1, ob)
+                result = small.tile([P, N], F32, name="result")
+                nc.vector.tensor_tensor(result[:], h1[ob][:], step[:], ALU.add)
+                nc.sync.dma_start(out[ob * P : (ob + 1) * P, :], result[:])

@@ -18,16 +18,28 @@ N = 256
 A = 64
 Q = N // A
 XYZ = 3
-PAIRS = A * N
 BANK = 512
-CHUNKS = PAIRS // BANK
 VMAX = 8.0
 GAMMA = 1.0 / (VMAX / K) ** 2
 EPS = 1e-6
-HALF = PAIRS // 2
-ROWS = 8
+ROWS = 16
+BLOCKS = A // ROWS
+SUMMED = 8
+FOLD = BANK // (SUMMED * Q)
 
-FLOPS = 2 * (2 * K * C * PAIRS + 2 * C * C * N)
+FLOPS = 2 * (2 * K * C * A * N + 2 * C * C * N)
+
+
+def kept(b):
+    return Q * (A - ROWS * b)
+
+
+def first_pair(b):
+    return sum(ROWS * kept(earlier) for earlier in range(b))
+
+
+def rows_in_bank(b):
+    return BANK // kept(b)
 
 
 def tile_crystalencoder_b_kernel(
@@ -43,20 +55,23 @@ def tile_crystalencoder_b_kernel(
         edge_b = [held.tile([P, CB], F32, name=f"edge_b{l}") for l in range(2)]
         node_b = [held.tile([P, CB], F32, name=f"node_b{l}") for l in range(2)]
         tables = [held.tile([P, S], F32, name=f"table{cb}") for cb in range(CB)]
-        rbf = held.tile([K, PAIRS], BF16, name="rbf")
+        rbf = held.tile([K, first_pair(BLOCKS)], BF16, name="rbf")
         h1 = [held.tile([P, N], F32, name=f"h1_{cb}") for cb in range(CB)]
+        agg = [held.tile([P, CB, N], BF16, name=f"agg{l}") for l in range(2)]
         one = held.tile([P, 1], F32, name="one")
         nc.vector.memset(one[:], 1.0)
+        identity = held.tile([P, P], F32, name="identity")
+        make_identity(nc, identity[:])
 
         with (
             tc.tile_pool(name="geometry", bufs=1) as geometry,
             tc.tile_pool(name="squares", bufs=2) as squares,
             tc.psum_pool(name="spread", bufs=2) as spread,
         ):
-            atoms = geometry.tile([CHUNKS, XYZ * N], F32, name="atoms")
-            nc.sync.dma_start(atoms[:], cart.rearrange("e t -> (e t)").partition_broadcast(CHUNKS))
-            partners = geometry.tile([CHUNKS, XYZ * Q, 2], F32, name="partners")
-            nc.sync.dma_start(partners[:], cart.rearrange("e (q i a) -> i (e q) a", q=Q, i=CHUNKS, a=2))
+            atoms = geometry.tile([A // 2, XYZ * N], F32, name="atoms")
+            nc.sync.dma_start(atoms[:], cart.rearrange("e t -> (e t)").partition_broadcast(A // 2))
+            partners = geometry.tile([A // 2, XYZ * Q, 2], F32, name="partners")
+            nc.sync.dma_start(partners[:], cart.rearrange("e (q i a) -> i (e q) a", q=Q, i=A // 2, a=2))
 
             for l, (w, b, nw, nb) in enumerate(
                 ((edge_w0, edge_b0, node_w0, node_b0), (edge_w1, edge_b1, node_w1, node_b1))
@@ -70,116 +85,160 @@ def tile_crystalencoder_b_kernel(
                 queue = nc.sync if cb % 2 == 0 else nc.gpsimd
                 queue.dma_start(tables[cb][:], table[cb * P : (cb + 1) * P, :])
 
-            identity = geometry.tile([P, P], F32, name="identity")
-            make_identity(nc, identity[:])
-            pick = geometry.tile([P, CHUNKS, P], F32, name="pick")
-            nc.vector.tensor_copy(pick[:], identity[:, 0:CHUNKS].unsqueeze(2).to_broadcast([P, CHUNKS, P]))
+            pick = geometry.tile([P, A // 2, P], F32, name="pick")
+            nc.vector.tensor_copy(pick[:], identity[:, 0 : A // 2].unsqueeze(2).to_broadcast([P, A // 2, P]))
             basis_index = geometry.tile([K, 1], I32, name="basis_index")
             nc.gpsimd.iota(basis_index[:], pattern=[[0, 1]], base=0, channel_multiplier=1)
             minus_center = geometry.tile([K, 1], F32, name="minus_center")
             nc.vector.tensor_scalar_mul(minus_center[:], basis_index[:], -VMAX / (K - 1))
 
-            diff = geometry.tile([CHUNKS, 2, XYZ * Q, A], F32, name="diff")
+            diff = geometry.tile([A // 2, 2, XYZ * Q, A], F32, name="diff")
             for a in range(2):
                 nc.vector.tensor_tensor(
                     diff[:, a],
                     atoms[:].rearrange("p (g j) -> p g j", j=A),
-                    partners[:, :, a : a + 1].to_broadcast([CHUNKS, XYZ * Q, A]),
+                    partners[:, :, a : a + 1].to_broadcast([A // 2, XYZ * Q, A]),
                     ALU.subtract,
                 )
             nc.vector.tensor_tensor(diff[:], diff[:], diff[:], ALU.mult)
             square = diff[:].rearrange("p a (e q) j -> p a e (q j)", e=XYZ)
             dist = geometry.tile([P, 2, N], F32, name="dist")
             nc.vector.memset(dist[:], 0.0)
-            nc.vector.tensor_tensor(dist[0:CHUNKS], square[:, :, 0], square[:, :, 1], ALU.add)
+            nc.vector.tensor_tensor(dist[0 : A // 2], square[:, :, 0], square[:, :, 1], ALU.add)
             nc.vector.scalar_tensor_tensor(
-                dist[0:CHUNKS], dist[0:CHUNKS], EPS, square[:, :, 2], op0=ALU.add, op1=ALU.add
+                dist[0 : A // 2], dist[0 : A // 2], EPS, square[:, :, 2], op0=ALU.add, op1=ALU.add
             )
-            nc.scalar.activation(dist[0:CHUNKS], dist[0:CHUNKS], ACT.Sqrt)
+            nc.scalar.activation(dist[0 : A // 2], dist[0 : A // 2], ACT.Sqrt)
 
-            for g in range(CHUNKS // 4):
-                gap2 = squares.tile([K, 4 * BANK], F32, name="gap2")
-                for u in range(4):
+            for b in range(BLOCKS):
+                two_rows = dist[:].rearrange("p a (q j) -> p (a q) j", j=A)[:, :, ROWS * b :]
+                columns = rows_in_bank(b) * kept(b)
+                for u in range(ROWS // rows_in_bank(b)):
                     d_everywhere = spread.tile([K, BANK], F32, name="d_everywhere")
-                    nc.tensor.matmul(
-                        d_everywhere[:],
-                        pick[:, 4 * g + u, :],
-                        dist[:].rearrange("p a t -> p (a t)"),
-                        start=True,
-                        stop=True,
-                    )
+                    for m in range(rows_in_bank(b) // 2):
+                        i = (ROWS * b + rows_in_bank(b) * u) // 2 + m
+                        nc.tensor.matmul(
+                            d_everywhere[:, 2 * kept(b) * m : 2 * kept(b) * (m + 1)],
+                            pick[:, i, :],
+                            two_rows,
+                            start=True,
+                            stop=True,
+                        )
+                    gap2 = squares.tile([K, BANK], F32, name="gap2")
                     nc.scalar.activation(
-                        gap2[:, u * BANK : (u + 1) * BANK], d_everywhere[:], ACT.Square, bias=minus_center[:]
+                        gap2[:, 0:columns], d_everywhere[:, 0:columns], ACT.Square, bias=minus_center[:]
                     )
-                nc.scalar.activation(rbf[:, g * 4 * BANK : (g + 1) * 4 * BANK], gap2[:], ACT.Exp, scale=-GAMMA)
+                    first = first_pair(b) + u * columns
+                    nc.scalar.activation(rbf[:, first : first + columns], gap2[:, 0:columns], ACT.Exp, scale=-GAMMA)
 
         with (
-            tc.tile_pool(name="gates", bufs=2) as gates,
+            tc.tile_pool(name="gates", bufs=7) as gates,
             tc.tile_pool(name="products", bufs=2) as products,
             tc.tile_pool(name="small", bufs=2) as small,
-            tc.psum_pool(name="banks", bufs=6) as banks,
+            tc.psum_pool(name="banks", bufs=4) as banks,
+            tc.psum_pool(name="folds", bufs=2) as folds,
             tc.psum_pool(name="node", bufs=2) as node,
         ):
 
-            def make_gates(l, cb, half):
-                gate = gates.tile([P, HALF], F32, name="gate")
-                for u in range(HALF // BANK):
-                    first = half * HALF + u * BANK
-                    pre = banks.tile([P, BANK], F32, name="pre")
-                    nc.tensor.matmul(
-                        pre[:], edge_w[l][:, cb * P : (cb + 1) * P], rbf[:, first : first + BANK], start=True, stop=True
-                    )
-                    nc.scalar.activation(
-                        gate[:, u * BANK : (u + 1) * BANK], pre[:], ACT.Exp, bias=edge_b[l][:, cb : cb + 1]
-                    )
-                for g in range(HALF // (ROWS * N)):
-                    rows = gate[:, g * ROWS * N : (g + 1) * ROWS * N]
-                    nc.scalar.activation(rows, rows, ACT.Ln, bias=one[:])
+            def by_crystal(block):
+                return block[:].rearrange("p r (q j) -> p r q j", j=A)
+
+            def make_gates(l, cb):
+                gate = [gates.tile([P, ROWS, N], F32, name=f"gate{b}", tag="gate") for b in range(BLOCKS)]
+                for b in range(BLOCKS):
+                    columns = rows_in_bank(b) * kept(b)
+                    for u in range(ROWS // rows_in_bank(b)):
+                        first = first_pair(b) + u * columns
+                        pre = banks.tile([P, BANK], F32, name="pre")
+                        nc.tensor.matmul(
+                            pre[:, 0:columns],
+                            edge_w[l][:, cb * P : (cb + 1) * P],
+                            rbf[:, first : first + columns],
+                            start=True,
+                            stop=True,
+                        )
+                        nc.scalar.activation(
+                            by_crystal(gate[b])[:, rows_in_bank(b) * u : rows_in_bank(b) * (u + 1), :, ROWS * b :],
+                            pre[:, 0:columns].rearrange("p (r q j) -> p r q j", r=rows_in_bank(b), q=Q),
+                            ACT.Exp,
+                            bias=edge_b[l][:, cb : cb + 1],
+                        )
+                for b in range(BLOCKS):
+                    for earlier in range(b):
+                        nc.scalar.copy(
+                            by_crystal(gate[b])[:, :, :, ROWS * earlier : ROWS * (earlier + 1)],
+                            by_crystal(gate[earlier])[:, :, :, ROWS * b : ROWS * (b + 1)].rearrange(
+                                "p r q j -> p j q r"
+                            ),
+                        )
+                    computed = by_crystal(gate[b])[:, :, :, ROWS * b :]
+                    nc.scalar.activation(computed, computed, ACT.Ln, bias=one[:])
                 return gate
 
-            def sum_over_partners(sums, first_rho, product):
-                nc.vector.tensor_reduce(
-                    sums[:, first_rho : first_rho + ROWS, :],
-                    product[:].rearrange("p a (q j) -> p a q j", j=A),
-                    axis=AXIS.X,
-                    op=ALU.add,
-                )
-
-            def to_list_order(agg, cb, sums):
+            def to_list_order(l, cb, sums):
                 nc.vector.tensor_copy(
-                    agg[:, cb, :].rearrange("p (q r) -> p q r", q=Q), sums[:].rearrange("p r q -> p q r")
+                    agg[l][:, cb, :].rearrange("p (q r) -> p q r", q=Q), sums.rearrange("p (r q) -> p q r", q=Q)
                 )
 
-            def node_update(l, agg, ob):
+            def node_update(l, ob):
                 z = node.tile([P, N], F32, name="z")
                 for mb in range(CB):
                     nc.tensor.matmul(
-                        z[:], node_w[l][:, mb, ob * P : (ob + 1) * P], agg[:, mb, :], start=(mb == 0), stop=(mb == CB - 1)
+                        z[:],
+                        node_w[l][:, mb, ob * P : (ob + 1) * P],
+                        agg[l][:, mb, :],
+                        start=(mb == 0),
+                        stop=(mb == CB - 1),
                     )
                 step = small.tile([P, N], F32, name="step")
                 nc.scalar.activation(step[:], z[:], ACT.Silu, bias=node_b[l][:, ob : ob + 1])
                 return step
 
-            agg0 = held.tile([P, CB, N], BF16, name="agg0")
+            def looked_up_times_gate0(cb, b, gate, sums):
+                for half in range(ROWS // SUMMED):
+                    product = products.tile([P, SUMMED, N], F32, name="product")
+                    for r in range(SUMMED):
+                        nc.vector.tensor_tensor(
+                            product[:, r, :],
+                            tables[cb][:].indirect(offsets[:]),
+                            gate[:, SUMMED * half + r, :],
+                            ALU.mult,
+                        )
+                    folded = folds.tile([P, SUMMED * Q, FOLD], F32, name="folded")
+                    for i in range(A // FOLD):
+                        nc.tensor.matmul(
+                            folded[:],
+                            identity[:],
+                            product[:].rearrange("p r (q j) -> p (r q) j", j=A)[:, :, FOLD * i : FOLD * (i + 1)],
+                            start=(i == 0),
+                            stop=(i == A // FOLD - 1),
+                        )
+                    first = (ROWS * b + SUMMED * half) * Q
+                    nc.vector.tensor_reduce(sums[:, first : first + SUMMED * Q], folded[:], axis=AXIS.X, op=ALU.add)
+
+            def h1_times_gate1(cb, b, gate, sums):
+                nc.vector.tensor_tensor(
+                    gate[:], gate[:], h1[cb][:].unsqueeze(1).to_broadcast([P, ROWS, N]), ALU.mult
+                )
+                nc.vector.tensor_reduce(
+                    sums[:, ROWS * Q * b : ROWS * Q * (b + 1)],
+                    gate[:].rearrange("p r (q j) -> p (r q) j", j=A),
+                    axis=AXIS.X,
+                    op=ALU.add,
+                )
+
+            gate = make_gates(0, 0)
             for cb in range(CB):
-                sums = small.tile([P, A, Q], F32, name="sums")
-                for half in range(2):
-                    gate = make_gates(0, cb, half)
-                    for g in range(HALF // (ROWS * N)):
-                        product = products.tile([P, ROWS, N], F32, name="product")
-                        for a in range(ROWS):
-                            row = g * ROWS + a
-                            nc.vector.tensor_tensor(
-                                product[:, a, :],
-                                tables[cb][:].indirect(offsets[:]),
-                                gate[:, row * N : (row + 1) * N],
-                                ALU.mult,
-                            )
-                        sum_over_partners(sums, half * (A // 2) + g * ROWS, product)
-                to_list_order(agg0, cb, sums)
+                sums = small.tile([P, A * Q], F32, name="sums")
+                looked_up_times_gate0(cb, 0, gate[0], sums)
+                upcoming = make_gates(0, cb + 1) if cb + 1 < CB else make_gates(1, 0)
+                for b in range(1, BLOCKS):
+                    looked_up_times_gate0(cb, b, gate[b], sums)
+                to_list_order(0, cb, sums[:])
+                gate = upcoming
 
             for ob in range(CB):
-                step = node_update(0, agg0, ob)
+                step = node_update(0, ob)
                 for piece in range(2):
                     entries = slice(piece * (N // 2), (piece + 1) * (N // 2))
                     nc.vector.tensor_tensor(
@@ -189,24 +248,18 @@ def tile_crystalencoder_b_kernel(
                         ALU.add,
                     )
 
-            agg1 = held.tile([P, CB, N], BF16, name="agg1")
             for cb in range(CB):
-                sums = small.tile([P, A, Q], F32, name="sums")
-                for half in range(2):
-                    gate = make_gates(1, cb, half)
-                    for g in range(HALF // (ROWS * N)):
-                        product = products.tile([P, ROWS, N], F32, name="product")
-                        nc.vector.tensor_tensor(
-                            product[:],
-                            gate[:, g * ROWS * N : (g + 1) * ROWS * N].rearrange("p (a t) -> p a t", t=N),
-                            h1[cb][:].unsqueeze(1).to_broadcast([P, ROWS, N]),
-                            ALU.mult,
-                        )
-                        sum_over_partners(sums, half * (A // 2) + g * ROWS, product)
-                to_list_order(agg1, cb, sums)
+                sums = small.tile([P, A * Q], F32, name="sums")
+                h1_times_gate1(cb, 0, gate[0], sums)
+                if cb + 1 < CB:
+                    upcoming = make_gates(1, cb + 1)
+                for b in range(1, BLOCKS):
+                    h1_times_gate1(cb, b, gate[b], sums)
+                to_list_order(1, cb, sums[:])
+                gate = upcoming
 
             for ob in range(CB):
-                step = node_update(1, agg1, ob)
+                step = node_update(1, ob)
                 result = small.tile([P, N], F32, name="result")
                 nc.vector.tensor_tensor(result[:], h1[ob][:], step[:], ALU.add)
                 nc.sync.dma_start(out[ob * P : (ob + 1) * P, :], result[:])

@@ -26,6 +26,7 @@ ROWS = 16
 BLOCKS = A // ROWS
 SUMMED = 8
 FOLD = BANK // (SUMMED * Q)
+TWO_ROWS = A // 2
 
 FLOPS = 2 * (2 * K * C * A * N + 2 * C * C * N)
 
@@ -68,47 +69,47 @@ def tile_crystalencoder_b_kernel(
             tc.tile_pool(name="squares", bufs=2) as squares,
             tc.psum_pool(name="spread", bufs=2) as spread,
         ):
-            atoms = geometry.tile([A // 2, XYZ * N], F32, name="atoms")
-            nc.sync.dma_start(atoms[:], cart.rearrange("e t -> (e t)").partition_broadcast(A // 2))
-            partners = geometry.tile([A // 2, XYZ * Q, 2], F32, name="partners")
-            nc.sync.dma_start(partners[:], cart.rearrange("e (q i a) -> i (e q) a", q=Q, i=A // 2, a=2))
+            atoms = geometry.tile([TWO_ROWS, XYZ * N], F32, name="atoms")
+            nc.sync.dma_start(atoms[:], cart.rearrange("e t -> (e t)").partition_broadcast(TWO_ROWS))
+            partners = geometry.tile([TWO_ROWS, XYZ * Q, 2], F32, name="partners")
+            nc.sync.dma_start(partners[:], cart.rearrange("e (q i a) -> i (e q) a", q=Q, i=TWO_ROWS, a=2))
 
-            for l, (w, b, nw, nb) in enumerate(
+            for l, (ew, eb, nw, nb) in enumerate(
                 ((edge_w0, edge_b0, node_w0, node_b0), (edge_w1, edge_b1, node_w1, node_b1))
             ):
-                nc.scalar.dma_start(edge_w[l][:], w)
+                nc.scalar.dma_start(edge_w[l][:], ew)
                 nc.scalar.dma_start(node_w[l][:], nw.rearrange("(m p) c -> p m c", p=P))
                 with nc.allow_non_contiguous_dma(reason="one bias value to a partition"):
-                    nc.scalar.dma_start(edge_b[l][:], b.rearrange("(a p) o -> p (a o)", p=P))
+                    nc.scalar.dma_start(edge_b[l][:], eb.rearrange("(a p) o -> p (a o)", p=P))
                     nc.scalar.dma_start(node_b[l][:], nb.rearrange("(a p) o -> p (a o)", p=P))
             for cb in range(CB):
                 queue = nc.sync if cb % 2 == 0 else nc.gpsimd
                 queue.dma_start(tables[cb][:], table[cb * P : (cb + 1) * P, :])
 
-            pick = geometry.tile([P, A // 2, P], F32, name="pick")
-            nc.vector.tensor_copy(pick[:], identity[:, 0 : A // 2].unsqueeze(2).to_broadcast([P, A // 2, P]))
+            pick = geometry.tile([P, TWO_ROWS, P], F32, name="pick")
+            nc.vector.tensor_copy(pick[:], identity[:, 0:TWO_ROWS].unsqueeze(2).to_broadcast([P, TWO_ROWS, P]))
             basis_index = geometry.tile([K, 1], I32, name="basis_index")
             nc.gpsimd.iota(basis_index[:], pattern=[[0, 1]], base=0, channel_multiplier=1)
             minus_center = geometry.tile([K, 1], F32, name="minus_center")
             nc.vector.tensor_scalar_mul(minus_center[:], basis_index[:], -VMAX / (K - 1))
 
-            diff = geometry.tile([A // 2, 2, XYZ * Q, A], F32, name="diff")
+            diff = geometry.tile([TWO_ROWS, 2, XYZ * Q, A], F32, name="diff")
             for a in range(2):
                 nc.vector.tensor_tensor(
                     diff[:, a],
                     atoms[:].rearrange("p (g j) -> p g j", j=A),
-                    partners[:, :, a : a + 1].to_broadcast([A // 2, XYZ * Q, A]),
+                    partners[:, :, a : a + 1].to_broadcast([TWO_ROWS, XYZ * Q, A]),
                     ALU.subtract,
                 )
             nc.vector.tensor_tensor(diff[:], diff[:], diff[:], ALU.mult)
             square = diff[:].rearrange("p a (e q) j -> p a e (q j)", e=XYZ)
             dist = geometry.tile([P, 2, N], F32, name="dist")
             nc.vector.memset(dist[:], 0.0)
-            nc.vector.tensor_tensor(dist[0 : A // 2], square[:, :, 0], square[:, :, 1], ALU.add)
+            nc.vector.tensor_tensor(dist[0:TWO_ROWS], square[:, :, 0], square[:, :, 1], ALU.add)
             nc.vector.scalar_tensor_tensor(
-                dist[0 : A // 2], dist[0 : A // 2], EPS, square[:, :, 2], op0=ALU.add, op1=ALU.add
+                dist[0:TWO_ROWS], dist[0:TWO_ROWS], EPS, square[:, :, 2], op0=ALU.add, op1=ALU.add
             )
-            nc.scalar.activation(dist[0 : A // 2], dist[0 : A // 2], ACT.Sqrt)
+            nc.scalar.activation(dist[0:TWO_ROWS], dist[0:TWO_ROWS], ACT.Sqrt)
 
             for b in range(BLOCKS):
                 two_rows = dist[:].rearrange("p a (q j) -> p (a q) j", j=A)[:, :, ROWS * b :]
@@ -116,10 +117,9 @@ def tile_crystalencoder_b_kernel(
                 for u in range(ROWS // rows_in_bank(b)):
                     d_everywhere = spread.tile([K, BANK], F32, name="d_everywhere")
                     for m in range(rows_in_bank(b) // 2):
-                        i = (ROWS * b + rows_in_bank(b) * u) // 2 + m
                         nc.tensor.matmul(
                             d_everywhere[:, 2 * kept(b) * m : 2 * kept(b) * (m + 1)],
-                            pick[:, i, :],
+                            pick[:, (ROWS * b + rows_in_bank(b) * u) // 2 + m, :],
                             two_rows,
                             start=True,
                             stop=True,
@@ -128,12 +128,12 @@ def tile_crystalencoder_b_kernel(
                     nc.scalar.activation(
                         gap2[:, 0:columns], d_everywhere[:, 0:columns], ACT.Square, bias=minus_center[:]
                     )
-                    first = first_pair(b) + u * columns
-                    nc.scalar.activation(rbf[:, first : first + columns], gap2[:, 0:columns], ACT.Exp, scale=-GAMMA)
+                    pair = first_pair(b) + u * columns
+                    nc.scalar.activation(rbf[:, pair : pair + columns], gap2[:, 0:columns], ACT.Exp, scale=-GAMMA)
 
         with (
-            tc.tile_pool(name="gates", bufs=7) as gates,
-            tc.tile_pool(name="products", bufs=2) as products,
+            tc.tile_pool(name="gates", bufs=6) as gates,
+            tc.tile_pool(name="products", bufs=4) as products,
             tc.tile_pool(name="small", bufs=2) as small,
             tc.psum_pool(name="banks", bufs=4) as banks,
             tc.psum_pool(name="folds", bufs=2) as folds,
@@ -148,12 +148,12 @@ def tile_crystalencoder_b_kernel(
                 for b in range(BLOCKS):
                     columns = rows_in_bank(b) * kept(b)
                     for u in range(ROWS // rows_in_bank(b)):
-                        first = first_pair(b) + u * columns
+                        pair = first_pair(b) + u * columns
                         pre = banks.tile([P, BANK], F32, name="pre")
                         nc.tensor.matmul(
                             pre[:, 0:columns],
                             edge_w[l][:, cb * P : (cb + 1) * P],
-                            rbf[:, first : first + columns],
+                            rbf[:, pair : pair + columns],
                             start=True,
                             stop=True,
                         )
@@ -175,9 +175,52 @@ def tile_crystalencoder_b_kernel(
                     nc.scalar.activation(computed, computed, ACT.Ln, bias=one[:])
                 return gate
 
+            def sum_with_tensor(product, sums, s):
+                folded = folds.tile([P, SUMMED * Q, FOLD], F32, name="folded")
+                for f in range(A // FOLD):
+                    nc.tensor.matmul(
+                        folded[:],
+                        identity[:],
+                        product[:].rearrange("p r (q j) -> p (r q) j", j=A)[:, :, FOLD * f : FOLD * (f + 1)],
+                        start=(f == 0),
+                        stop=(f == A // FOLD - 1),
+                    )
+                nc.vector.tensor_reduce(sums[:, s : s + SUMMED * Q], folded[:], axis=AXIS.X, op=ALU.add)
+
+            def sum_on_vector(product, sums, s):
+                nc.vector.tensor_reduce(
+                    sums[:, s : s + SUMMED * Q],
+                    product[:].rearrange("p r (q j) -> p (r q) j", j=A),
+                    axis=AXIS.X,
+                    op=ALU.add,
+                )
+
+            def looked_up_times_gate0(cb, b, gate, sums):
+                for half in range(ROWS // SUMMED):
+                    product = products.tile([P, SUMMED, N], F32, name="product")
+                    for r in range(SUMMED):
+                        nc.vector.tensor_tensor(
+                            product[:, r, :],
+                            tables[cb][:].indirect(offsets[:]),
+                            gate[:, SUMMED * half + r, :],
+                            ALU.mult,
+                        )
+                    sum_with_tensor(product, sums, (ROWS * b + SUMMED * half) * Q)
+
+            def h1_times_gate1(cb, b, gate, sums):
+                for half in range(ROWS // SUMMED):
+                    product = products.tile([P, SUMMED, N], F32, name="product")
+                    nc.vector.tensor_tensor(
+                        product[:],
+                        gate[:, SUMMED * half : SUMMED * (half + 1), :],
+                        h1[cb][:].unsqueeze(1).to_broadcast([P, SUMMED, N]),
+                        ALU.mult,
+                    )
+                    sum_on_vector(product, sums, (ROWS * b + SUMMED * half) * Q)
+
             def to_list_order(l, cb, sums):
                 nc.vector.tensor_copy(
-                    agg[l][:, cb, :].rearrange("p (q r) -> p q r", q=Q), sums.rearrange("p (r q) -> p q r", q=Q)
+                    agg[l][:, cb, :].rearrange("p (q r) -> p q r", q=Q), sums[:].rearrange("p (r q) -> p q r", q=Q)
                 )
 
             def node_update(l, ob):
@@ -194,39 +237,6 @@ def tile_crystalencoder_b_kernel(
                 nc.scalar.activation(step[:], z[:], ACT.Silu, bias=node_b[l][:, ob : ob + 1])
                 return step
 
-            def looked_up_times_gate0(cb, b, gate, sums):
-                for half in range(ROWS // SUMMED):
-                    product = products.tile([P, SUMMED, N], F32, name="product")
-                    for r in range(SUMMED):
-                        nc.vector.tensor_tensor(
-                            product[:, r, :],
-                            tables[cb][:].indirect(offsets[:]),
-                            gate[:, SUMMED * half + r, :],
-                            ALU.mult,
-                        )
-                    folded = folds.tile([P, SUMMED * Q, FOLD], F32, name="folded")
-                    for i in range(A // FOLD):
-                        nc.tensor.matmul(
-                            folded[:],
-                            identity[:],
-                            product[:].rearrange("p r (q j) -> p (r q) j", j=A)[:, :, FOLD * i : FOLD * (i + 1)],
-                            start=(i == 0),
-                            stop=(i == A // FOLD - 1),
-                        )
-                    first = (ROWS * b + SUMMED * half) * Q
-                    nc.vector.tensor_reduce(sums[:, first : first + SUMMED * Q], folded[:], axis=AXIS.X, op=ALU.add)
-
-            def h1_times_gate1(cb, b, gate, sums):
-                nc.vector.tensor_tensor(
-                    gate[:], gate[:], h1[cb][:].unsqueeze(1).to_broadcast([P, ROWS, N]), ALU.mult
-                )
-                nc.vector.tensor_reduce(
-                    sums[:, ROWS * Q * b : ROWS * Q * (b + 1)],
-                    gate[:].rearrange("p r (q j) -> p (r q) j", j=A),
-                    axis=AXIS.X,
-                    op=ALU.add,
-                )
-
             gate = make_gates(0, 0)
             for cb in range(CB):
                 sums = small.tile([P, A * Q], F32, name="sums")
@@ -234,7 +244,7 @@ def tile_crystalencoder_b_kernel(
                 upcoming = make_gates(0, cb + 1) if cb + 1 < CB else make_gates(1, 0)
                 for b in range(1, BLOCKS):
                     looked_up_times_gate0(cb, b, gate[b], sums)
-                to_list_order(0, cb, sums[:])
+                to_list_order(0, cb, sums)
                 gate = upcoming
 
             for ob in range(CB):
@@ -251,11 +261,10 @@ def tile_crystalencoder_b_kernel(
             for cb in range(CB):
                 sums = small.tile([P, A * Q], F32, name="sums")
                 h1_times_gate1(cb, 0, gate[0], sums)
-                if cb + 1 < CB:
-                    upcoming = make_gates(1, cb + 1)
+                upcoming = make_gates(1, cb + 1) if cb + 1 < CB else None
                 for b in range(1, BLOCKS):
                     h1_times_gate1(cb, b, gate[b], sums)
-                to_list_order(1, cb, sums[:])
+                to_list_order(1, cb, sums)
                 gate = upcoming
 
             for ob in range(CB):

@@ -22,32 +22,28 @@ BANK = 512
 VMAX = 8.0
 GAMMA = 1.0 / (VMAX / K) ** 2
 EPS = 1e-6
-ROWS = 16
-BLOCKS = A // ROWS
-SUMMED = 8
-FOLD = BANK // (SUMMED * Q)
-TWO_ROWS = A // 2
+HALF = A // 2
+SHIFTS = HALF + 1
+PAIR = BANK // N
+CHUNK = 4
+AHEAD = 5
 
 FLOPS = 2 * (2 * K * C * A * N + 2 * C * C * N)
 
 
-def kept(b):
-    return Q * (A - ROWS * b)
-
-
-def first_pair(b):
-    return sum(ROWS * kept(earlier) for earlier in range(b))
-
-
-def rows_in_bank(b):
-    return BANK // kept(b)
+def banks_of_rows():
+    return [(s, min(PAIR, SHIFTS - s)) for s in range(0, SHIFTS, PAIR)]
 
 
 def tile_crystalencoder_b_kernel(
     tc, table, cart, edge_w0, edge_b0, node_w0, node_b0, edge_w1, edge_b1, node_w1, node_b1, offs, out
 ):
     nc = tc.nc
-    with tc.tile_pool(name="held", bufs=1) as held:
+    with (
+        tc.tile_pool(name="held", bufs=1) as held,
+        tc.tile_pool(name="gates", bufs=2) as gates,
+        tc.psum_pool(name="banks", bufs=4) as banks,
+    ):
         offsets = held.tile([P, N // 16], U16, name="offsets")
         nc.sync.dma_start(offsets[:], offs)
 
@@ -56,219 +52,246 @@ def tile_crystalencoder_b_kernel(
         edge_b = [held.tile([P, CB], F32, name=f"edge_b{l}") for l in range(2)]
         node_b = [held.tile([P, CB], F32, name=f"node_b{l}") for l in range(2)]
         tables = [held.tile([P, S], F32, name=f"table{cb}") for cb in range(CB)]
-        rbf = held.tile([K, first_pair(BLOCKS)], BF16, name="rbf")
-        h1 = [held.tile([P, N], F32, name=f"h1_{cb}") for cb in range(CB)]
+        rbf = held.tile([K, SHIFTS, Q, A], BF16, name="rbf")
+        h1 = [held.tile([P, Q, A], F32, name=f"h1_{cb}") for cb in range(CB)]
+        h1_around = [held.tile([P, Q, HALF + A], F32, name=f"h1_around{cb}") for cb in range(CB)]
         agg = [held.tile([P, CB, N], BF16, name=f"agg{l}") for l in range(2)]
-        one = held.tile([P, 1], F32, name="one")
-        nc.vector.memset(one[:], 1.0)
         identity = held.tile([P, P], F32, name="identity")
         make_identity(nc, identity[:])
+        zeros = held.tile([P, Q, 2 * A], BF16, name="zeros")
+        nc.vector.memset(zeros[:], 0.0)
+        identity_bf16 = held.tile([P, P], BF16, name="identity_bf16")
+        make_identity(nc, identity_bf16[:])
 
         with (
             tc.tile_pool(name="geometry", bufs=1) as geometry,
-            tc.tile_pool(name="squares", bufs=2) as squares,
+            tc.tile_pool(name="stream", bufs=3) as stream,
             tc.psum_pool(name="spread", bufs=2) as spread,
         ):
-            atoms = geometry.tile([TWO_ROWS, XYZ * N], F32, name="atoms")
-            nc.sync.dma_start(atoms[:], cart.rearrange("e t -> (e t)").partition_broadcast(TWO_ROWS))
-            partners = geometry.tile([TWO_ROWS, XYZ * Q, 2], F32, name="partners")
-            nc.sync.dma_start(partners[:], cart.rearrange("e (q i a) -> i (e q) a", q=Q, i=TWO_ROWS, a=2))
+            atoms = geometry.tile([P, XYZ * N], F32, name="atoms")
+            nc.sync.dma_start(atoms[:], cart.rearrange("e t -> (e t)").partition_broadcast(P))
+            own = geometry.tile([P, 2, 8], F32, name="own")
+            with nc.allow_non_contiguous_dma(reason="one atom's three coordinates to a partition"):
+                for q in range(Q):
+                    a, b = divmod(q, 2)
+                    nc.sync.dma_start(
+                        own[a * A : (a + 1) * A, b, 0:XYZ], cart[:, A * q : A * (q + 1)].rearrange("e r -> r e")
+                    )
 
-            for l, (ew, eb, nw, nb) in enumerate(
-                ((edge_w0, edge_b0, node_w0, node_b0), (edge_w1, edge_b1, node_w1, node_b1))
-            ):
-                nc.scalar.dma_start(edge_w[l][:], ew)
-                nc.scalar.dma_start(node_w[l][:], nw.rearrange("(m p) c -> p m c", p=P))
+            def load_bias(queue, tile, bias):
                 with nc.allow_non_contiguous_dma(reason="one bias value to a partition"):
-                    nc.scalar.dma_start(edge_b[l][:], eb.rearrange("(a p) o -> p (a o)", p=P))
-                    nc.scalar.dma_start(node_b[l][:], nb.rearrange("(a p) o -> p (a o)", p=P))
+                    queue.dma_start(tile[:], bias.rearrange("(a p) o -> p (a o)", p=P))
+
+            nc.sync.dma_start(edge_w[0][:], edge_w0)
+            load_bias(nc.sync, edge_b[0], edge_b0)
             for cb in range(CB):
                 queue = nc.sync if cb % 2 == 0 else nc.gpsimd
                 queue.dma_start(tables[cb][:], table[cb * P : (cb + 1) * P, :])
+            nc.sync.dma_start(node_w[0][:], node_w0.rearrange("(m p) c -> p m c", p=P))
+            load_bias(nc.sync, node_b[0], node_b0)
+            nc.gpsimd.dma_start(edge_w[1][:], edge_w1)
+            load_bias(nc.gpsimd, edge_b[1], edge_b1)
+            nc.gpsimd.dma_start(node_w[1][:], node_w1.rearrange("(m p) c -> p m c", p=P))
+            load_bias(nc.gpsimd, node_b[1], node_b1)
 
-            pick = geometry.tile([P, TWO_ROWS, P], F32, name="pick")
-            nc.vector.tensor_copy(pick[:], identity[:, 0:TWO_ROWS].unsqueeze(2).to_broadcast([P, TWO_ROWS, P]))
+            is_atom = geometry.tile([P, A], F32, name="is_atom")
+            nc.vector.tensor_tensor(is_atom[:], identity[:, 0:A], identity[:, A : 2 * A], ALU.add)
+            side = [geometry.tile([P, K], F32, name=f"side{a}") for a in range(2)]
+            for a in range(2):
+                nc.vector.memset(side[a][:], 0.0)
+                nc.vector.memset(side[a][a * A : (a + 1) * A, :], 1.0)
             basis_index = geometry.tile([K, 1], I32, name="basis_index")
             nc.gpsimd.iota(basis_index[:], pattern=[[0, 1]], base=0, channel_multiplier=1)
             minus_center = geometry.tile([K, 1], F32, name="minus_center")
             nc.vector.tensor_scalar_mul(minus_center[:], basis_index[:], -VMAX / (K - 1))
 
-            diff = geometry.tile([TWO_ROWS, 2, XYZ * Q, A], F32, name="diff")
+            diff = geometry.tile([P, 2, XYZ, A], F32, name="diff")
             for a in range(2):
+                half = slice(a * A, (a + 1) * A)
                 nc.vector.tensor_tensor(
-                    diff[:, a],
-                    atoms[:].rearrange("p (g j) -> p g j", j=A),
-                    partners[:, :, a : a + 1].to_broadcast([TWO_ROWS, XYZ * Q, A]),
+                    diff[half],
+                    atoms[half]
+                    .rearrange("p (e t) -> p e t", e=XYZ)[:, :, 2 * A * a : 2 * A * (a + 1)]
+                    .rearrange("p e (b j) -> p b e j", b=2),
+                    own[half, :, 0:XYZ].unsqueeze(3).to_broadcast([A, 2, XYZ, A]),
                     ALU.subtract,
                 )
             nc.vector.tensor_tensor(diff[:], diff[:], diff[:], ALU.mult)
-            square = diff[:].rearrange("p a (e q) j -> p a e (q j)", e=XYZ)
-            dist = geometry.tile([P, 2, N], F32, name="dist")
-            nc.vector.memset(dist[:], 0.0)
-            nc.vector.tensor_tensor(dist[0:TWO_ROWS], square[:, :, 0], square[:, :, 1], ALU.add)
-            nc.vector.scalar_tensor_tensor(
-                dist[0:TWO_ROWS], dist[0:TWO_ROWS], EPS, square[:, :, 2], op0=ALU.add, op1=ALU.add
-            )
-            nc.scalar.activation(dist[0:TWO_ROWS], dist[0:TWO_ROWS], ACT.Sqrt)
+            dist2 = geometry.tile([P, 2, A], F32, name="dist2")
+            nc.vector.tensor_tensor(dist2[:], diff[:, :, 0], diff[:, :, 1], ALU.add)
+            nc.vector.scalar_tensor_tensor(dist2[:], dist2[:], EPS, diff[:, :, 2], op0=ALU.add, op1=ALU.add)
+            dist_around = geometry.tile([P, 2, HALF + A], F32, name="dist_around")
+            nc.scalar.activation(dist_around[:, :, HALF : HALF + A], dist2[:], ACT.Sqrt)
+            nc.scalar.activation(dist_around[:, :, 0:HALF], dist2[:, :, HALF:A], ACT.Sqrt)
 
-            for b in range(BLOCKS):
-                two_rows = dist[:].rearrange("p a (q j) -> p (a q) j", j=A)[:, :, ROWS * b :]
-                columns = rows_in_bank(b) * kept(b)
-                for u in range(ROWS // rows_in_bank(b)):
-                    d_everywhere = spread.tile([K, BANK], F32, name="d_everywhere")
-                    for m in range(rows_in_bank(b) // 2):
-                        nc.tensor.matmul(
-                            d_everywhere[:, 2 * kept(b) * m : 2 * kept(b) * (m + 1)],
-                            pick[:, (ROWS * b + rows_in_bank(b) * u) // 2 + m, :],
-                            two_rows,
-                            start=True,
-                            stop=True,
-                        )
-                    gap2 = squares.tile([K, BANK], F32, name="gap2")
-                    nc.scalar.activation(
-                        gap2[:, 0:columns], d_everywhere[:, 0:columns], ACT.Square, bias=minus_center[:]
+            for s0, rows in banks_of_rows():
+                lone = stream.tile([P, PAIR, 2, A], F32, name="lone")
+                for i in range(rows):
+                    first = HALF - (s0 + i)
+                    nc.vector.tensor_tensor(
+                        lone[:, i],
+                        dist_around[:, :, first : first + A],
+                        is_atom[:].unsqueeze(1).to_broadcast([P, 2, A]),
+                        ALU.mult,
                     )
-                    pair = first_pair(b) + u * columns
-                    nc.scalar.activation(rbf[:, pair : pair + columns], gap2[:, 0:columns], ACT.Exp, scale=-GAMMA)
+                d_everywhere = spread.tile([K, PAIR, Q, A], F32, name="d_everywhere")
+                for a in range(2):
+                    nc.tensor.matmul(
+                        d_everywhere[:, 0:rows, 2 * a : 2 * a + 2, :], side[a][:], lone[:, 0:rows], start=True, stop=True
+                    )
+                gap2 = stream.tile([K, PAIR, Q, A], F32, name="gap2")
+                nc.scalar.activation(gap2[:, 0:rows], d_everywhere[:, 0:rows], ACT.Square, bias=minus_center[:])
+                nc.scalar.activation(rbf[:, s0 : s0 + rows], gap2[:, 0:rows], ACT.Exp, scale=-GAMMA)
 
         with (
-            tc.tile_pool(name="gates", bufs=6) as gates,
-            tc.tile_pool(name="products", bufs=4) as products,
+            tc.tile_pool(name="products", bufs=8) as products,
+            tc.tile_pool(name="turns", bufs=AHEAD + 2) as turns,
             tc.tile_pool(name="small", bufs=2) as small,
-            tc.psum_pool(name="banks", bufs=4) as banks,
-            tc.psum_pool(name="folds", bufs=2) as folds,
+            tc.psum_pool(name="sums", bufs=2) as sums,
             tc.psum_pool(name="node", bufs=2) as node,
         ):
 
-            def by_crystal(block):
-                return block[:].rearrange("p r (q j) -> p r q j", j=A)
-
-            def make_gates(l, cb):
-                gate = [gates.tile([P, ROWS, N], F32, name=f"gate{b}", tag="gate") for b in range(BLOCKS)]
-                for b in range(BLOCKS):
-                    columns = rows_in_bank(b) * kept(b)
-                    for u in range(ROWS // rows_in_bank(b)):
-                        pair = first_pair(b) + u * columns
-                        pre = banks.tile([P, BANK], F32, name="pre")
-                        nc.tensor.matmul(
-                            pre[:, 0:columns],
-                            edge_w[l][:, cb * P : (cb + 1) * P],
-                            rbf[:, pair : pair + columns],
-                            start=True,
-                            stop=True,
-                        )
-                        nc.scalar.activation(
-                            by_crystal(gate[b])[:, rows_in_bank(b) * u : rows_in_bank(b) * (u + 1), :, ROWS * b :],
-                            pre[:, 0:columns].rearrange("p (r q j) -> p r q j", r=rows_in_bank(b), q=Q),
-                            ACT.Exp,
-                            bias=edge_b[l][:, cb : cb + 1],
-                        )
-                for b in range(BLOCKS):
-                    for earlier in range(b):
-                        nc.scalar.copy(
-                            by_crystal(gate[b])[:, :, :, ROWS * earlier : ROWS * (earlier + 1)],
-                            by_crystal(gate[earlier])[:, :, :, ROWS * b : ROWS * (b + 1)].rearrange(
-                                "p r q j -> p j q r"
-                            ),
-                        )
-                    computed = by_crystal(gate[b])[:, :, :, ROWS * b :]
-                    nc.scalar.activation(computed, computed, ACT.Ln, bias=one[:])
-                return gate
-
-            def sum_with_tensor(product, sums, s):
-                folded = folds.tile([P, SUMMED * Q, FOLD], F32, name="folded")
-                for f in range(A // FOLD):
+            def exponentials(l, cb, gate, some_banks):
+                for s0, rows in some_banks:
+                    pre = banks.tile([P, PAIR, Q, A], F32, name="pre")
                     nc.tensor.matmul(
-                        folded[:],
-                        identity[:],
-                        product[:].rearrange("p r (q j) -> p (r q) j", j=A)[:, :, FOLD * f : FOLD * (f + 1)],
-                        start=(f == 0),
-                        stop=(f == A // FOLD - 1),
+                        pre[:, 0:rows], edge_w[l][:, cb * P : (cb + 1) * P], rbf[:, s0 : s0 + rows], start=True, stop=True
                     )
-                nc.vector.tensor_reduce(sums[:, s : s + SUMMED * Q], folded[:], axis=AXIS.X, op=ALU.add)
-
-            def sum_on_vector(product, sums, s):
-                nc.vector.tensor_reduce(
-                    sums[:, s : s + SUMMED * Q],
-                    product[:].rearrange("p r (q j) -> p (r q) j", j=A),
-                    axis=AXIS.X,
-                    op=ALU.add,
-                )
-
-            def looked_up_times_gate0(cb, b, gate, sums):
-                for half in range(ROWS // SUMMED):
-                    product = products.tile([P, SUMMED, N], F32, name="product")
-                    for r in range(SUMMED):
-                        nc.vector.tensor_tensor(
-                            product[:, r, :],
-                            tables[cb][:].indirect(offsets[:]),
-                            gate[:, SUMMED * half + r, :],
-                            ALU.mult,
-                        )
-                    sum_with_tensor(product, sums, (ROWS * b + SUMMED * half) * Q)
-
-            def h1_times_gate1(cb, b, gate, sums):
-                for half in range(ROWS // SUMMED):
-                    product = products.tile([P, SUMMED, N], F32, name="product")
-                    nc.vector.tensor_tensor(
-                        product[:],
-                        gate[:, SUMMED * half : SUMMED * (half + 1), :],
-                        h1[cb][:].unsqueeze(1).to_broadcast([P, SUMMED, N]),
-                        ALU.mult,
+                    nc.scalar.activation(
+                        gate[:, s0 : s0 + rows], pre[:, 0:rows], ACT.Exp, bias=edge_b[l][:, cb : cb + 1]
                     )
-                    sum_on_vector(product, sums, (ROWS * b + SUMMED * half) * Q)
 
-            def to_list_order(l, cb, sums):
-                nc.vector.tensor_copy(
-                    agg[l][:, cb, :].rearrange("p (q r) -> p q r", q=Q), sums[:].rearrange("p (r q) -> p q r", q=Q)
-                )
+            def logarithm(gate):
+                one_at_last = small.tile([P, 1], F32, name="one_at_last")
+                nc.scalar.activation(one_at_last[:], gate[:, SHIFTS - 1, Q - 1, A - 1 : A], ACT.Copy, bias=1.0, scale=0.0)
+                for s0 in range(0, SHIFTS, SHIFTS // 3):
+                    piece = gate[:, s0 : s0 + SHIFTS // 3]
+                    nc.scalar.activation(piece, piece, ACT.Ln, bias=one_at_last[:])
+
+            def turn(gate, step):
+                turned = turns.tile([P, 2, Q, A], F32, name="turned")
+                for i in range(2):
+                    s = 2 * step + i
+                    if s > 0:
+                        nc.scalar.copy(turned[:, i, :, 0 : A - s], gate[:, s, :, s:A])
+                        nc.scalar.copy(turned[:, i, :, A - s : A], gate[:, s, :, 0:s])
+                return turned
+
+            def empty_total():
+                total = sums.tile([P, Q, 2 * A], F32, name="total")
+                nc.tensor.matmul(total[:], identity_bf16[:], zeros[:], start=True, stop=False)
+                return total
+
+            def add_shifted(total, row, right, stop=False):
+                nc.tensor.matmul(total[:, :, right : right + A], identity[:], row, start=False, stop=stop)
+
+            def looked_up_times_gate0(cb, step, gate, turned, total):
+                product = products.tile([P, CHUNK, Q, A], F32, name="product")
+                forward = [2 * step, 2 * step + 1]
+                backward = [2 * step + 1, 2 * step + 2]
+                partners = [turned[:, s % 2] if s > 0 else gate[:, 0] for s in forward] + [gate[:, s] for s in backward]
+                rights = forward + [A - s for s in backward]
+                for i in range(CHUNK):
+                    nc.vector.tensor_tensor(product[:, i], tables[cb][:].indirect(offsets[:]), partners[i], ALU.mult)
+                for i in range(CHUNK):
+                    add_shifted(total, product[:, i], rights[i], stop=(backward[1] == HALF and i == CHUNK - 1))
+
+            def round_to_agg(l, cb, total):
+                both = small.tile([P, Q, A], F32, name="both")
+                nc.vector.tensor_reduce(both[:], total[:].rearrange("p q (h r) -> p q r h", h=2), axis=AXIS.X, op=ALU.add)
+                nc.vector.tensor_copy(agg[l][:, cb, :], both[:].rearrange("p q r -> p (q r)"))
 
             def node_update(l, ob):
-                z = node.tile([P, N], F32, name="z")
+                z = node.tile([P, Q, A], F32, name="z")
                 for mb in range(CB):
                     nc.tensor.matmul(
-                        z[:],
+                        z[:].rearrange("p q r -> p (q r)"),
                         node_w[l][:, mb, ob * P : (ob + 1) * P],
                         agg[l][:, mb, :],
                         start=(mb == 0),
                         stop=(mb == CB - 1),
                     )
-                step = small.tile([P, N], F32, name="step")
-                nc.scalar.activation(step[:], z[:], ACT.Silu, bias=node_b[l][:, ob : ob + 1])
-                return step
+                update = small.tile([P, Q, A], F32, name="update")
+                nc.scalar.activation(update[:], z[:], ACT.Silu, bias=node_b[l][:, ob : ob + 1])
+                return update
 
-            gate = make_gates(0, 0)
+            every_bank = banks_of_rows()
+
+            steps = HALF // 2
+            gate = gates.tile([P, SHIFTS, Q, A], F32, name="gate", tag="gate")
+            exponentials(0, 0, gate, every_bank)
+            logarithm(gate)
+            turned = {}
+            for step in range(AHEAD):
+                turned[(0, step)] = turn(gate, step)
             for cb in range(CB):
-                sums = small.tile([P, A * Q], F32, name="sums")
-                looked_up_times_gate0(cb, 0, gate[0], sums)
-                upcoming = make_gates(0, cb + 1) if cb + 1 < CB else make_gates(1, 0)
-                for b in range(1, BLOCKS):
-                    looked_up_times_gate0(cb, b, gate[b], sums)
-                to_list_order(0, cb, sums)
+                l_next, cb_next = (0, cb + 1) if cb + 1 < CB else (1, 0)
+                upcoming = gates.tile([P, SHIFTS, Q, A], F32, name="upcoming", tag="gate")
+                total = empty_total()
+                for step in range(steps):
+                    later = step + AHEAD
+                    if later < steps:
+                        turned[(cb, later)] = turn(gate, later)
+                    elif cb + 1 < CB:
+                        turned[(cb + 1, later - steps)] = turn(upcoming, later - steps)
+                    looked_up_times_gate0(cb, step, gate, turned[(cb, step)], total)
+                    some_banks = every_bank[2 * step : 2 * step + 2]
+                    exponentials(l_next, cb_next, upcoming, some_banks)
+                    if some_banks and some_banks[-1] == every_bank[-1]:
+                        logarithm(upcoming)
+                round_to_agg(0, cb, total)
                 gate = upcoming
 
             for ob in range(CB):
-                step = node_update(0, ob)
+                update = node_update(0, ob)
                 for piece in range(2):
-                    entries = slice(piece * (N // 2), (piece + 1) * (N // 2))
+                    crystals = slice(piece * (Q // 2), (piece + 1) * (Q // 2))
                     nc.vector.tensor_tensor(
-                        h1[ob][:, entries],
+                        h1[ob][:, crystals],
                         tables[ob][:].indirect(offsets[:, piece * (N // 32) : (piece + 1) * (N // 32)]),
-                        step[:, entries],
+                        update[:, crystals],
                         ALU.add,
                     )
+                nc.vector.tensor_copy(h1_around[ob][:, :, 0:HALF], h1[ob][:, :, HALF:A])
+                nc.vector.tensor_copy(h1_around[ob][:, :, HALF : HALF + A], h1[ob][:])
 
+            steps = HALF // CHUNK
             for cb in range(CB):
-                sums = small.tile([P, A * Q], F32, name="sums")
-                h1_times_gate1(cb, 0, gate[0], sums)
-                upcoming = make_gates(1, cb + 1) if cb + 1 < CB else None
-                for b in range(1, BLOCKS):
-                    h1_times_gate1(cb, b, gate[b], sums)
-                to_list_order(1, cb, sums)
+                if cb + 1 < CB:
+                    upcoming = gates.tile([P, SHIFTS, Q, A], F32, name="upcoming", tag="gate")
+                total = empty_total()
+                two_columns = total[:].rearrange("p q (h r) -> p h q r", h=2)
+                forward = []
+                for step in range(steps + 1):
+                    if step < steps:
+                        ahead = products.tile([P, CHUNK, Q, A], F32, name="ahead", tag="product")
+                        back = products.tile([P, CHUNK, Q, A], F32, name="back", tag="product")
+                        for i in range(CHUNK):
+                            s = CHUNK * step + i
+                            nc.vector.tensor_tensor(
+                                ahead[:, i], gate[:, s], h1_around[cb][:, :, HALF - s : HALF - s + A], ALU.mult
+                            )
+                        for i in range(CHUNK):
+                            nc.vector.tensor_tensor(back[:, i], gate[:, CHUNK * step + i + 1], h1[cb][:], ALU.mult)
+                        for i in range(CHUNK):
+                            add_shifted(total, back[:, i], A - (CHUNK * step + i + 1))
+                        forward.append(ahead)
+                    if step % 2 == 1:
+                        nc.vector.tensor_tensor(forward[step - 1][:], forward[step - 1][:], forward[step][:], ALU.add)
+                    if step % 2 == 0 and step > 0:
+                        eight = forward[step - 2]
+                        nc.vector.tensor_tensor(eight[:, 0:2], eight[:, 0:2], eight[:, 2:4], ALU.add)
+                        nc.tensor.matmul(two_columns, identity[:], eight[:, 0:2], start=False, stop=(step == steps))
+                    if cb + 1 < CB:
+                        some_banks = every_bank[5 * step : 5 * step + 5]
+                        exponentials(1, cb + 1, upcoming, some_banks)
+                        if some_banks and some_banks[-1] == every_bank[-1]:
+                            logarithm(upcoming)
+                round_to_agg(1, cb, total)
                 gate = upcoming
 
             for ob in range(CB):
-                step = node_update(1, ob)
-                result = small.tile([P, N], F32, name="result")
-                nc.vector.tensor_tensor(result[:], h1[ob][:], step[:], ALU.add)
-                nc.sync.dma_start(out[ob * P : (ob + 1) * P, :], result[:])
+                update = node_update(1, ob)
+                result = small.tile([P, Q, A], F32, name="result")
+                nc.vector.tensor_tensor(result[:], h1[ob][:], update[:], ALU.add)
+                nc.sync.dma_start(out[ob * P : (ob + 1) * P, :], result[:].rearrange("p q r -> p (q r)"))

@@ -25,8 +25,9 @@ EPS = 1e-6
 HALF = A // 2
 SHIFTS = HALF + 1
 PAIR = BANK // N
+THIRD = SHIFTS // 3
 CHUNK = 4
-AHEAD = 5
+AHEAD = 10
 
 FLOPS = 2 * (2 * K * C * A * N + 2 * C * C * N)
 
@@ -54,7 +55,6 @@ def tile_crystalencoder_b_kernel(
         tables = [held.tile([P, S], F32, name=f"table{cb}") for cb in range(CB)]
         rbf = held.tile([K, SHIFTS, Q, A], BF16, name="rbf")
         h1 = [held.tile([P, Q, A], F32, name=f"h1_{cb}") for cb in range(CB)]
-        h1_around = [held.tile([P, Q, HALF + A], F32, name=f"h1_around{cb}") for cb in range(CB)]
         agg = [held.tile([P, CB, N], BF16, name=f"agg{l}") for l in range(2)]
         identity = held.tile([P, P], F32, name="identity")
         make_identity(nc, identity[:])
@@ -139,16 +139,18 @@ def tile_crystalencoder_b_kernel(
                     nc.tensor.matmul(
                         d_everywhere[:, 0:rows, 2 * a : 2 * a + 2, :], side[a][:], lone[:, 0:rows], start=True, stop=True
                     )
+                gap = stream.tile([K, PAIR, Q, A], F32, name="gap")
+                nc.vector.tensor_scalar_add(gap[:, 0:rows], d_everywhere[:, 0:rows], minus_center[:])
                 gap2 = stream.tile([K, PAIR, Q, A], F32, name="gap2")
-                nc.scalar.activation(gap2[:, 0:rows], d_everywhere[:, 0:rows], ACT.Square, bias=minus_center[:])
+                nc.vector.tensor_tensor(gap2[:, 0:rows], gap[:, 0:rows], gap[:, 0:rows], ALU.mult)
                 nc.scalar.activation(rbf[:, s0 : s0 + rows], gap2[:, 0:rows], ACT.Exp, scale=-GAMMA)
 
         with (
-            tc.tile_pool(name="products", bufs=8) as products,
+            tc.tile_pool(name="products", bufs=10) as products,
             tc.tile_pool(name="turns", bufs=AHEAD + 2) as turns,
             tc.tile_pool(name="small", bufs=2) as small,
             tc.psum_pool(name="sums", bufs=2) as sums,
-            tc.psum_pool(name="node", bufs=2) as node,
+            tc.psum_pool(name="around", bufs=2) as around,
         ):
 
             def exponentials(l, cb, gate, some_banks):
@@ -161,12 +163,19 @@ def tile_crystalencoder_b_kernel(
                         gate[:, s0 : s0 + rows], pre[:, 0:rows], ACT.Exp, bias=edge_b[l][:, cb : cb + 1]
                     )
 
-            def logarithm(gate):
+            def one_after_exponentials(gate):
                 one_at_last = small.tile([P, 1], F32, name="one_at_last")
                 nc.scalar.activation(one_at_last[:], gate[:, SHIFTS - 1, Q - 1, A - 1 : A], ACT.Copy, bias=1.0, scale=0.0)
-                for s0 in range(0, SHIFTS, SHIFTS // 3):
-                    piece = gate[:, s0 : s0 + SHIFTS // 3]
-                    nc.scalar.activation(piece, piece, ACT.Ln, bias=one_at_last[:])
+                return one_at_last
+
+            def logarithm(gate, third, one_at_last):
+                rows = gate[:, third * THIRD : (third + 1) * THIRD]
+                nc.scalar.activation(rows, rows, ACT.Ln, bias=one_at_last[:])
+
+            def logarithms(gate):
+                one_at_last = one_after_exponentials(gate)
+                for third in range(SHIFTS // THIRD):
+                    logarithm(gate, third, one_at_last)
 
             def turn(gate, step):
                 turned = turns.tile([P, 2, Q, A], F32, name="turned")
@@ -202,7 +211,7 @@ def tile_crystalencoder_b_kernel(
                 nc.vector.tensor_copy(agg[l][:, cb, :], both[:].rearrange("p q r -> p (q r)"))
 
             def node_update(l, ob):
-                z = node.tile([P, Q, A], F32, name="z")
+                z = sums.tile([P, Q, A], F32, name="z", tag="total")
                 for mb in range(CB):
                     nc.tensor.matmul(
                         z[:].rearrange("p q r -> p (q r)"),
@@ -220,10 +229,13 @@ def tile_crystalencoder_b_kernel(
             steps = HALF // 2
             gate = gates.tile([P, SHIFTS, Q, A], F32, name="gate", tag="gate")
             exponentials(0, 0, gate, every_bank)
-            logarithm(gate)
+            one_at_last = one_after_exponentials(gate)
             turned = {}
-            for step in range(AHEAD):
-                turned[(0, step)] = turn(gate, step)
+            for third in range(SHIFTS // THIRD):
+                logarithm(gate, third, one_at_last)
+                for step in range(AHEAD):
+                    if (2 * step + 1) // THIRD == third:
+                        turned[(0, step)] = turn(gate, step)
             for cb in range(CB):
                 l_next, cb_next = (0, cb + 1) if cb + 1 < CB else (1, 0)
                 upcoming = gates.tile([P, SHIFTS, Q, A], F32, name="upcoming", tag="gate")
@@ -235,10 +247,10 @@ def tile_crystalencoder_b_kernel(
                     elif cb + 1 < CB:
                         turned[(cb + 1, later - steps)] = turn(upcoming, later - steps)
                     looked_up_times_gate0(cb, step, gate, turned[(cb, step)], total)
-                    some_banks = every_bank[2 * step : 2 * step + 2]
+                    some_banks = every_bank[3 * step : 3 * step + 3]
                     exponentials(l_next, cb_next, upcoming, some_banks)
                     if some_banks and some_banks[-1] == every_bank[-1]:
-                        logarithm(upcoming)
+                        logarithms(upcoming)
                 round_to_agg(0, cb, total)
                 gate = upcoming
 
@@ -252,41 +264,42 @@ def tile_crystalencoder_b_kernel(
                         update[:, crystals],
                         ALU.add,
                     )
-                nc.vector.tensor_copy(h1_around[ob][:, :, 0:HALF], h1[ob][:, :, HALF:A])
-                nc.vector.tensor_copy(h1_around[ob][:, :, HALF : HALF + A], h1[ob][:])
 
             steps = HALF // CHUNK
             for cb in range(CB):
                 if cb + 1 < CB:
                     upcoming = gates.tile([P, SHIFTS, Q, A], F32, name="upcoming", tag="gate")
+                h1_around = around.tile([P, Q, HALF + A], F32, name="h1_around")
+                nc.tensor.matmul(h1_around[:, :, 0:HALF], identity[:], h1[cb][:, :, HALF:A], start=True, stop=True)
+                nc.tensor.matmul(h1_around[:, :, HALF : HALF + A], identity[:], h1[cb][:], start=True, stop=True)
                 total = empty_total()
-                two_columns = total[:].rearrange("p q (h r) -> p h q r", h=2)
-                forward = []
-                for step in range(steps + 1):
-                    if step < steps:
-                        ahead = products.tile([P, CHUNK, Q, A], F32, name="ahead", tag="product")
-                        back = products.tile([P, CHUNK, Q, A], F32, name="back", tag="product")
-                        for i in range(CHUNK):
-                            s = CHUNK * step + i
-                            nc.vector.tensor_tensor(
-                                ahead[:, i], gate[:, s], h1_around[cb][:, :, HALF - s : HALF - s + A], ALU.mult
-                            )
-                        for i in range(CHUNK):
-                            nc.vector.tensor_tensor(back[:, i], gate[:, CHUNK * step + i + 1], h1[cb][:], ALU.mult)
-                        for i in range(CHUNK):
-                            add_shifted(total, back[:, i], A - (CHUNK * step + i + 1))
-                        forward.append(ahead)
-                    if step % 2 == 1:
-                        nc.vector.tensor_tensor(forward[step - 1][:], forward[step - 1][:], forward[step][:], ALU.add)
-                    if step % 2 == 0 and step > 0:
-                        eight = forward[step - 2]
-                        nc.vector.tensor_tensor(eight[:, 0:2], eight[:, 0:2], eight[:, 2:4], ALU.add)
-                        nc.tensor.matmul(two_columns, identity[:], eight[:, 0:2], start=False, stop=(step == steps))
+                for step in range(steps):
+                    forward = products.tile([P, CHUNK, Q, A], F32, name="forward", tag="product")
+                    backward = products.tile([P, CHUNK, Q, A], F32, name="backward", tag="product")
+                    for i in range(CHUNK):
+                        s = CHUNK * step + i
+                        nc.vector.tensor_tensor(forward[:, i], gate[:, s], h1_around[:, :, HALF - s : HALF - s + A], ALU.mult)
+                    s0 = CHUNK * step + 1
+                    nc.vector.tensor_tensor(
+                        backward[:],
+                        gate[:, s0 : s0 + CHUNK],
+                        h1_around[:, :, HALF : HALF + A].unsqueeze(1).to_broadcast([P, CHUNK, Q, A]),
+                        ALU.mult,
+                    )
+                    for i in range(CHUNK):
+                        add_shifted(total, backward[:, i], A - (s0 + i))
+                    if step == 0:
+                        four_rows = forward
+                    else:
+                        nc.gpsimd.tensor_tensor(four_rows[:], four_rows[:], forward[:], ALU.add)
                     if cb + 1 < CB:
                         some_banks = every_bank[5 * step : 5 * step + 5]
                         exponentials(1, cb + 1, upcoming, some_banks)
                         if some_banks and some_banks[-1] == every_bank[-1]:
-                            logarithm(upcoming)
+                            logarithms(upcoming)
+                two_columns = total[:].rearrange("p q (h r) -> p h q r", h=2)
+                nc.tensor.matmul(two_columns, identity[:], four_rows[:, 0:2], start=False, stop=False)
+                nc.tensor.matmul(two_columns, identity[:], four_rows[:, 2:4], start=False, stop=True)
                 round_to_agg(1, cb, total)
                 gate = upcoming
 

@@ -27,7 +27,7 @@ SHIFTS = HALF + 1
 PAIR = BANK // N
 THIRD = SHIFTS // 3
 CHUNK = 4
-AHEAD = 10
+AHEAD = 11
 
 FLOPS = 2 * (2 * K * C * A * N + 2 * C * C * N)
 
@@ -56,12 +56,31 @@ def tile_crystalencoder_b_kernel(
         rbf = held.tile([K, SHIFTS, Q, A], BF16, name="rbf")
         h1 = [held.tile([P, Q, A], F32, name=f"h1_{cb}") for cb in range(CB)]
         agg = [held.tile([P, CB, N], BF16, name=f"agg{l}") for l in range(2)]
+        basis_index = held.tile([K, 1], I32, name="basis_index")
+        nc.gpsimd.iota(basis_index[:], pattern=[[0, 1]], base=0, channel_multiplier=1)
+        minus_center = held.tile([K, 1], F32, name="minus_center")
+        nc.vector.tensor_scalar_mul(minus_center[:], basis_index[:], -VMAX / (K - 1))
         identity = held.tile([P, P], F32, name="identity")
         make_identity(nc, identity[:])
+
+        def load_table(func, after):
+            unread = held.tile([P, 1], F32, name="unread", tag="unread")
+            nc.scalar.activation(unread[:], after, func)
+
         zeros = held.tile([P, Q, 2 * A], BF16, name="zeros")
         nc.vector.memset(zeros[:], 0.0)
         identity_bf16 = held.tile([P, P], BF16, name="identity_bf16")
         make_identity(nc, identity_bf16[:])
+
+        def exponentials(l, cb, gate, some_banks):
+            for s0, rows in some_banks:
+                pre = banks.tile([P, PAIR, Q, A], F32, name="pre")
+                nc.tensor.matmul(
+                    pre[:, 0:rows], edge_w[l][:, cb * P : (cb + 1) * P], rbf[:, s0 : s0 + rows], start=True, stop=True
+                )
+                nc.scalar.activation(
+                    gate[:, s0 : s0 + rows], pre[:, 0:rows], ACT.Exp, bias=edge_b[l][:, cb : cb + 1]
+                )
 
         with (
             tc.tile_pool(name="geometry", bufs=1) as geometry,
@@ -85,14 +104,13 @@ def tile_crystalencoder_b_kernel(
             nc.sync.dma_start(edge_w[0][:], edge_w0)
             load_bias(nc.sync, edge_b[0], edge_b0)
             for cb in range(CB):
-                queue = nc.sync if cb % 2 == 0 else nc.gpsimd
-                queue.dma_start(tables[cb][:], table[cb * P : (cb + 1) * P, :])
+                nc.sync.dma_start(tables[cb][:], table[cb * P : (cb + 1) * P, :])
             nc.sync.dma_start(node_w[0][:], node_w0.rearrange("(m p) c -> p m c", p=P))
             load_bias(nc.sync, node_b[0], node_b0)
-            nc.gpsimd.dma_start(edge_w[1][:], edge_w1)
-            load_bias(nc.gpsimd, edge_b[1], edge_b1)
-            nc.gpsimd.dma_start(node_w[1][:], node_w1.rearrange("(m p) c -> p m c", p=P))
-            load_bias(nc.gpsimd, node_b[1], node_b1)
+            nc.sync.dma_start(edge_w[1][:], edge_w1)
+            load_bias(nc.sync, edge_b[1], edge_b1)
+            nc.sync.dma_start(node_w[1][:], node_w1.rearrange("(m p) c -> p m c", p=P))
+            load_bias(nc.sync, node_b[1], node_b1)
 
             is_atom = geometry.tile([P, A], F32, name="is_atom")
             nc.vector.tensor_tensor(is_atom[:], identity[:, 0:A], identity[:, A : 2 * A], ALU.add)
@@ -100,10 +118,6 @@ def tile_crystalencoder_b_kernel(
             for a in range(2):
                 nc.vector.memset(side[a][:], 0.0)
                 nc.vector.memset(side[a][a * A : (a + 1) * A, :], 1.0)
-            basis_index = geometry.tile([K, 1], I32, name="basis_index")
-            nc.gpsimd.iota(basis_index[:], pattern=[[0, 1]], base=0, channel_multiplier=1)
-            minus_center = geometry.tile([K, 1], F32, name="minus_center")
-            nc.vector.tensor_scalar_mul(minus_center[:], basis_index[:], -VMAX / (K - 1))
 
             diff = geometry.tile([P, 2, XYZ, A], F32, name="diff")
             for a in range(2):
@@ -124,6 +138,7 @@ def tile_crystalencoder_b_kernel(
             nc.scalar.activation(dist_around[:, :, HALF : HALF + A], dist2[:], ACT.Sqrt)
             nc.scalar.activation(dist_around[:, :, 0:HALF], dist2[:, :, HALF:A], ACT.Sqrt)
 
+            gate = gates.tile([P, SHIFTS, Q, A], F32, name="gate", tag="gate")
             for s0, rows in banks_of_rows():
                 lone = stream.tile([P, PAIR, 2, A], F32, name="lone")
                 for i in range(rows):
@@ -144,24 +159,15 @@ def tile_crystalencoder_b_kernel(
                 gap2 = stream.tile([K, PAIR, Q, A], F32, name="gap2")
                 nc.vector.tensor_tensor(gap2[:, 0:rows], gap[:, 0:rows], gap[:, 0:rows], ALU.mult)
                 nc.scalar.activation(rbf[:, s0 : s0 + rows], gap2[:, 0:rows], ACT.Exp, scale=-GAMMA)
+                exponentials(0, 0, gate, [(s0, rows)])
 
         with (
-            tc.tile_pool(name="products", bufs=10) as products,
+            tc.tile_pool(name="products", bufs=9) as products,
             tc.tile_pool(name="turns", bufs=AHEAD + 2) as turns,
-            tc.tile_pool(name="small", bufs=2) as small,
+            tc.tile_pool(name="small", bufs=CB) as small,
             tc.psum_pool(name="sums", bufs=2) as sums,
             tc.psum_pool(name="around", bufs=2) as around,
         ):
-
-            def exponentials(l, cb, gate, some_banks):
-                for s0, rows in some_banks:
-                    pre = banks.tile([P, PAIR, Q, A], F32, name="pre")
-                    nc.tensor.matmul(
-                        pre[:, 0:rows], edge_w[l][:, cb * P : (cb + 1) * P], rbf[:, s0 : s0 + rows], start=True, stop=True
-                    )
-                    nc.scalar.activation(
-                        gate[:, s0 : s0 + rows], pre[:, 0:rows], ACT.Exp, bias=edge_b[l][:, cb : cb + 1]
-                    )
 
             def one_after_exponentials(gate):
                 one_at_last = small.tile([P, 1], F32, name="one_at_last")
@@ -206,12 +212,16 @@ def tile_crystalencoder_b_kernel(
                     add_shifted(total, product[:, i], rights[i], stop=(backward[1] == HALF and i == CHUNK - 1))
 
             def round_to_agg(l, cb, total):
-                both = small.tile([P, Q, A], F32, name="both")
-                nc.vector.tensor_reduce(both[:], total[:].rearrange("p q (h r) -> p q r h", h=2), axis=AXIS.X, op=ALU.add)
-                nc.vector.tensor_copy(agg[l][:, cb, :], both[:].rearrange("p q r -> p (q r)"))
+                with nc.allow_low_precision(reason="the sum of two float32 values is rounded once, to agg's bfloat16"):
+                    nc.vector.tensor_reduce(
+                        agg[l][:, cb, :].rearrange("p (q r) -> p q r", q=Q),
+                        total[:].rearrange("p q (h r) -> p q r h", h=2),
+                        axis=AXIS.X,
+                        op=ALU.add,
+                    )
 
             def node_update(l, ob):
-                z = sums.tile([P, Q, A], F32, name="z", tag="total")
+                z = banks.tile([P, Q, A], F32, name="z", tag="pre")
                 for mb in range(CB):
                     nc.tensor.matmul(
                         z[:].rearrange("p q r -> p (q r)"),
@@ -227,8 +237,6 @@ def tile_crystalencoder_b_kernel(
             every_bank = banks_of_rows()
 
             steps = HALF // 2
-            gate = gates.tile([P, SHIFTS, Q, A], F32, name="gate", tag="gate")
-            exponentials(0, 0, gate, every_bank)
             one_at_last = one_after_exponentials(gate)
             turned = {}
             for third in range(SHIFTS // THIRD):
@@ -247,10 +255,12 @@ def tile_crystalencoder_b_kernel(
                     elif cb + 1 < CB:
                         turned[(cb + 1, later - steps)] = turn(upcoming, later - steps)
                     looked_up_times_gate0(cb, step, gate, turned[(cb, step)], total)
-                    some_banks = every_bank[3 * step : 3 * step + 3]
+                    some_banks = every_bank[4 * step : 4 * step + 4]
                     exponentials(l_next, cb_next, upcoming, some_banks)
                     if some_banks and some_banks[-1] == every_bank[-1]:
                         logarithms(upcoming)
+                        if cb == CB - 1:
+                            load_table(ACT.Silu, upcoming[:, SHIFTS - 1, Q - 1, A - 1 : A])
                 round_to_agg(0, cb, total)
                 gate = upcoming
 
@@ -297,6 +307,8 @@ def tile_crystalencoder_b_kernel(
                         exponentials(1, cb + 1, upcoming, some_banks)
                         if some_banks and some_banks[-1] == every_bank[-1]:
                             logarithms(upcoming)
+                            if cb + 1 == CB - 1:
+                                load_table(ACT.Silu, upcoming[:, SHIFTS - 1, Q - 1, A - 1 : A])
                 two_columns = total[:].rearrange("p q (h r) -> p h q r", h=2)
                 nc.tensor.matmul(two_columns, identity[:], four_rows[:, 0:2], start=False, stop=False)
                 nc.tensor.matmul(two_columns, identity[:], four_rows[:, 2:4], start=False, stop=True)

@@ -63,10 +63,6 @@ def tile_crystalencoder_b_kernel(
         identity = held.tile([P, P], F32, name="identity")
         make_identity(nc, identity[:])
 
-        def load_table(func, after):
-            unread = held.tile([P, 1], F32, name="unread", tag="unread")
-            nc.scalar.activation(unread[:], after, func)
-
         zeros = held.tile([P, Q, 2 * A], BF16, name="zeros")
         nc.vector.memset(zeros[:], 0.0)
         identity_bf16 = held.tile([P, P], BF16, name="identity_bf16")
@@ -259,8 +255,6 @@ def tile_crystalencoder_b_kernel(
                     exponentials(l_next, cb_next, upcoming, some_banks)
                     if some_banks and some_banks[-1] == every_bank[-1]:
                         logarithms(upcoming)
-                        if cb == CB - 1:
-                            load_table(ACT.Silu, upcoming[:, SHIFTS - 1, Q - 1, A - 1 : A])
                 round_to_agg(0, cb, total)
                 gate = upcoming
 
@@ -307,8 +301,6 @@ def tile_crystalencoder_b_kernel(
                         exponentials(1, cb + 1, upcoming, some_banks)
                         if some_banks and some_banks[-1] == every_bank[-1]:
                             logarithms(upcoming)
-                            if cb + 1 == CB - 1:
-                                load_table(ACT.Silu, upcoming[:, SHIFTS - 1, Q - 1, A - 1 : A])
                 two_columns = total[:].rearrange("p q (h r) -> p h q r", h=2)
                 nc.tensor.matmul(two_columns, identity[:], four_rows[:, 0:2], start=False, stop=False)
                 nc.tensor.matmul(two_columns, identity[:], four_rows[:, 2:4], start=False, stop=True)

@@ -277,6 +277,9 @@ def tile_crystalencoder_b_kernel(
                 nc.tensor.matmul(h1_around[:, :, 0:HALF], identity[:], h1[cb][:, :, HALF:A], start=True, stop=True)
                 nc.tensor.matmul(h1_around[:, :, HALF : HALF + A], identity[:], h1[cb][:], start=True, stop=True)
                 total = empty_total()
+                if cb + 1 < CB:
+                    exponentials(1, cb + 1, upcoming, every_bank)
+                    logarithms(upcoming)
                 for step in range(steps):
                     forward = products.tile([P, CHUNK, Q, A], F32, name="forward", tag="product")
                     backward = products.tile([P, CHUNK, Q, A], F32, name="backward", tag="product")
@@ -291,20 +294,18 @@ def tile_crystalencoder_b_kernel(
                         ALU.mult,
                     )
                     for i in range(CHUNK):
-                        add_shifted(total, backward[:, i], A - (s0 + i))
+                        add_shifted(total, backward[:, i], A - (s0 + i), stop=(s0 + i == HALF))
                     if step == 0:
                         four_rows = forward
                     else:
                         nc.gpsimd.tensor_tensor(four_rows[:], four_rows[:], forward[:], ALU.add)
-                    if cb + 1 < CB:
-                        some_banks = every_bank[5 * step : 5 * step + 5]
-                        exponentials(1, cb + 1, upcoming, some_banks)
-                        if some_banks and some_banks[-1] == every_bank[-1]:
-                            logarithms(upcoming)
-                two_columns = total[:].rearrange("p q (h r) -> p h q r", h=2)
-                nc.tensor.matmul(two_columns, identity[:], four_rows[:, 0:2], start=False, stop=False)
-                nc.tensor.matmul(two_columns, identity[:], four_rows[:, 2:4], start=False, stop=True)
-                round_to_agg(1, cb, total)
+                nc.gpsimd.tensor_tensor(four_rows[:, 0:2], four_rows[:, 0:2], four_rows[:, 2:4], ALU.add)
+                nc.gpsimd.tensor_tensor(four_rows[:, 0], four_rows[:, 0], four_rows[:, 1], ALU.add)
+                partial = small.tile([P, Q, A], F32, name="partial", tag="result")
+                nc.vector.tensor_tensor(partial[:], total[:, :, 0:A], four_rows[:, 0], ALU.add)
+                nc.vector.tensor_tensor(
+                    agg[1][:, cb, :].rearrange("p (q r) -> p q r", q=Q), total[:, :, A : 2 * A], partial[:], ALU.add
+                )
                 gate = upcoming
 
             for ob in range(CB):

@@ -26,6 +26,7 @@ HALF = A // 2
 SHIFTS = HALF + 1
 PAIR = BANK // N
 THIRD = SHIFTS // 3
+FIRST = 3
 CHUNK = 4
 AHEAD = 11
 
@@ -170,14 +171,14 @@ def tile_crystalencoder_b_kernel(
                 nc.scalar.activation(one_at_last[:], gate[:, SHIFTS - 1, Q - 1, A - 1 : A], ACT.Copy, bias=1.0, scale=0.0)
                 return one_at_last
 
-            def logarithm(gate, third, one_at_last):
-                rows = gate[:, third * THIRD : (third + 1) * THIRD]
+            def logarithm(gate, first_row, end_row, one_at_last):
+                rows = gate[:, first_row:end_row]
                 nc.scalar.activation(rows, rows, ACT.Ln, bias=one_at_last[:])
 
             def logarithms(gate):
                 one_at_last = one_after_exponentials(gate)
-                for third in range(SHIFTS // THIRD):
-                    logarithm(gate, third, one_at_last)
+                for first_row in range(0, SHIFTS, THIRD):
+                    logarithm(gate, first_row, first_row + THIRD, one_at_last)
 
             def turn(gate, step):
                 turned = turns.tile([P, 2, Q, A], F32, name="turned")
@@ -235,10 +236,11 @@ def tile_crystalencoder_b_kernel(
             steps = HALF // 2
             one_at_last = one_after_exponentials(gate)
             turned = {}
-            for third in range(SHIFTS // THIRD):
-                logarithm(gate, third, one_at_last)
+            cuts = [0, FIRST, THIRD, 2 * THIRD, SHIFTS]
+            for first_row, end_row in zip(cuts[:-1], cuts[1:]):
+                logarithm(gate, first_row, end_row, one_at_last)
                 for step in range(AHEAD):
-                    if (2 * step + 1) // THIRD == third:
+                    if first_row <= 2 * step + 1 < end_row:
                         turned[(0, step)] = turn(gate, step)
             for cb in range(CB):
                 l_next, cb_next = (0, cb + 1) if cb + 1 < CB else (1, 0)
@@ -271,6 +273,7 @@ def tile_crystalencoder_b_kernel(
 
             steps = HALF // CHUNK
             for cb in range(CB):
+                last_block = cb == CB - 1
                 if cb + 1 < CB:
                     upcoming = gates.tile([P, SHIFTS, Q, A], F32, name="upcoming", tag="gate")
                 h1_around = around.tile([P, Q, HALF + A], F32, name="h1_around")
@@ -298,9 +301,11 @@ def tile_crystalencoder_b_kernel(
                     if step == 0:
                         four_rows = forward
                     else:
-                        nc.gpsimd.tensor_tensor(four_rows[:], four_rows[:], forward[:], ALU.add)
-                nc.gpsimd.tensor_tensor(four_rows[:, 0:2], four_rows[:, 0:2], four_rows[:, 2:4], ALU.add)
-                nc.gpsimd.tensor_tensor(four_rows[:, 0], four_rows[:, 0], four_rows[:, 1], ALU.add)
+                        adder = nc.vector if last_block and step == steps - 1 else nc.gpsimd
+                        adder.tensor_tensor(four_rows[:], four_rows[:], forward[:], ALU.add)
+                folder = nc.vector if last_block else nc.gpsimd
+                folder.tensor_tensor(four_rows[:, 0:2], four_rows[:, 0:2], four_rows[:, 2:4], ALU.add)
+                folder.tensor_tensor(four_rows[:, 0], four_rows[:, 0], four_rows[:, 1], ALU.add)
                 partial = small.tile([P, Q, A], F32, name="partial", tag="result")
                 nc.vector.tensor_tensor(partial[:], total[:, :, 0:A], four_rows[:, 0], ALU.add)
                 nc.vector.tensor_tensor(

@@ -22,6 +22,8 @@ BANK = 512
 VMAX = 8.0
 GAMMA = 1.0 / (VMAX / K) ** 2
 EPS = 1e-6
+STEP = VMAX / (K - 1)
+MIDDLE = VMAX / 2
 HALF = A // 2
 SHIFTS = HALF + 1
 PAIR = BANK // N
@@ -47,7 +49,6 @@ def tile_crystalencoder_b_kernel(
         tc.psum_pool(name="banks", bufs=4) as banks,
     ):
         offsets = held.tile([P, N // 16], U16, name="offsets")
-        nc.sync.dma_start(offsets[:], offs)
 
         edge_w = [held.tile([K, C], BF16, name=f"edge_w{l}") for l in range(2)]
         node_w = [held.tile([P, CB, C], BF16, name=f"node_w{l}") for l in range(2)]
@@ -59,8 +60,19 @@ def tile_crystalencoder_b_kernel(
         agg = [held.tile([P, CB, N], BF16, name=f"agg{l}") for l in range(2)]
         basis_index = held.tile([K, 1], I32, name="basis_index")
         nc.gpsimd.iota(basis_index[:], pattern=[[0, 1]], base=0, channel_multiplier=1)
-        minus_center = held.tile([K, 1], F32, name="minus_center")
-        nc.vector.tensor_scalar_mul(minus_center[:], basis_index[:], -VMAX / (K - 1))
+        basis_along = held.tile([P, K], I32, name="basis_along")
+        nc.gpsimd.iota(basis_along[:], pattern=[[1, K]], base=0, channel_multiplier=0)
+        center = held.tile([K, 1], F32, name="center")
+        nc.vector.tensor_scalar(center[:], basis_index[:], STEP, -MIDDLE, op0=ALU.mult, op1=ALU.add)
+        minus_gamma_center2 = held.tile([K, 1], F32, name="minus_gamma_center2")
+        nc.vector.scalar_tensor_tensor(
+            minus_gamma_center2[:], center[:], -GAMMA, center[:], op0=ALU.mult, op1=ALU.mult
+        )
+        spread_w = held.tile([P, K], F32, name="spread_w")
+        nc.vector.tensor_scalar(spread_w[0:A], basis_along[0:A], STEP, -MIDDLE, op0=ALU.mult, op1=ALU.add)
+        nc.vector.memset(spread_w[A : 2 * A], -0.5)
+        minus_middle = held.tile([P, 1], F32, name="minus_middle")
+        nc.vector.memset(minus_middle[:], -MIDDLE)
         identity = held.tile([P, P], F32, name="identity")
         make_identity(nc, identity[:])
 
@@ -84,15 +96,15 @@ def tile_crystalencoder_b_kernel(
             tc.tile_pool(name="stream", bufs=3) as stream,
             tc.psum_pool(name="spread", bufs=2) as spread,
         ):
+            cart_rows = geometry.tile([XYZ * Q, 2 * A], F32, name="cart_rows")
+            for e in range(XYZ):
+                nc.sync.dma_start(
+                    cart_rows[e * Q : (e + 1) * Q].rearrange("p (u r) -> p u r", u=2),
+                    cart[e].rearrange("(q r) -> q r", q=Q).unsqueeze(1).to_broadcast([Q, 2, A]),
+                )
             atoms = geometry.tile([P, XYZ * N], F32, name="atoms")
             nc.sync.dma_start(atoms[:], cart.rearrange("e t -> (e t)").partition_broadcast(P))
-            own = geometry.tile([P, 2, 8], F32, name="own")
-            with nc.allow_non_contiguous_dma(reason="one atom's three coordinates to a partition"):
-                for q in range(Q):
-                    a, b = divmod(q, 2)
-                    nc.sync.dma_start(
-                        own[a * A : (a + 1) * A, b, 0:XYZ], cart[:, A * q : A * (q + 1)].rearrange("e r -> r e")
-                    )
+            nc.sync.dma_start(offsets[:], offs)
 
             def load_bias(queue, tile, bias):
                 with nc.allow_non_contiguous_dma(reason="one bias value to a partition"):
@@ -111,51 +123,48 @@ def tile_crystalencoder_b_kernel(
 
             is_atom = geometry.tile([P, A], F32, name="is_atom")
             nc.vector.tensor_tensor(is_atom[:], identity[:, 0:A], identity[:, A : 2 * A], ALU.add)
-            side = [geometry.tile([P, K], F32, name=f"side{a}") for a in range(2)]
-            for a in range(2):
-                nc.vector.memset(side[a][:], 0.0)
-                nc.vector.memset(side[a][a * A : (a + 1) * A, :], 1.0)
-
-            diff = geometry.tile([P, 2, XYZ, A], F32, name="diff")
-            for a in range(2):
-                half = slice(a * A, (a + 1) * A)
-                nc.vector.tensor_tensor(
-                    diff[half],
-                    atoms[half]
-                    .rearrange("p (e t) -> p e t", e=XYZ)[:, :, 2 * A * a : 2 * A * (a + 1)]
-                    .rearrange("p e (b j) -> p b e j", b=2),
-                    own[half, :, 0:XYZ].unsqueeze(3).to_broadcast([A, 2, XYZ, A]),
-                    ALU.subtract,
-                )
+            own = banks.tile([P, XYZ * Q], F32, name="own", tag="pre")
+            nc.tensor.matmul(own[:], cart_rows[:], identity[0 : XYZ * Q, 0 : XYZ * Q], start=True, stop=True)
+            diff = geometry.tile([P, XYZ * Q, A], F32, name="diff")
+            nc.vector.tensor_tensor(
+                diff[:],
+                atoms[:].rearrange("p (g j) -> p g j", j=A),
+                own[:].unsqueeze(2).to_broadcast([P, XYZ * Q, A]),
+                ALU.subtract,
+            )
             nc.vector.tensor_tensor(diff[:], diff[:], diff[:], ALU.mult)
-            dist2 = geometry.tile([P, 2, A], F32, name="dist2")
-            nc.vector.tensor_tensor(dist2[:], diff[:, :, 0], diff[:, :, 1], ALU.add)
-            nc.vector.scalar_tensor_tensor(dist2[:], dist2[:], EPS, diff[:, :, 2], op0=ALU.add, op1=ALU.add)
-            dist_around = geometry.tile([P, 2, HALF + A], F32, name="dist_around")
+            dist2 = geometry.tile([P, Q, A], F32, name="dist2")
+            nc.vector.tensor_tensor(dist2[:], diff[:, 0:Q], diff[:, Q : 2 * Q], ALU.add)
+            nc.vector.scalar_tensor_tensor(dist2[:], dist2[:], EPS, diff[:, 2 * Q : 3 * Q], op0=ALU.add, op1=ALU.add)
+            dist_around = geometry.tile([P, Q, HALF + A], F32, name="dist_around")
             nc.scalar.activation(dist_around[:, :, HALF : HALF + A], dist2[:], ACT.Sqrt)
             nc.scalar.activation(dist_around[:, :, 0:HALF], dist2[:, :, HALF:A], ACT.Sqrt)
+            t_around = geometry.tile([P, Q, HALF + A], F32, name="t_around")
+            nc.vector.tensor_scalar_add(t_around[0:A], dist_around[0:A], -MIDDLE)
+            nc.scalar.activation(
+                t_around[A : 2 * A], dist_around[A : 2 * A], ACT.Square, bias=minus_middle[A : 2 * A]
+            )
 
             gate = gates.tile([P, SHIFTS, Q, A], F32, name="gate", tag="gate")
             for s0, rows in banks_of_rows():
-                lone = stream.tile([P, PAIR, 2, A], F32, name="lone")
+                lone = stream.tile([P, PAIR, Q, A], F32, name="lone")
                 for i in range(rows):
                     first = HALF - (s0 + i)
                     nc.vector.tensor_tensor(
                         lone[:, i],
-                        dist_around[:, :, first : first + A],
-                        is_atom[:].unsqueeze(1).to_broadcast([P, 2, A]),
+                        t_around[:, :, first : first + A],
+                        is_atom[:].unsqueeze(1).to_broadcast([P, Q, A]),
                         ALU.mult,
                     )
-                d_everywhere = spread.tile([K, PAIR, Q, A], F32, name="d_everywhere")
-                for a in range(2):
-                    nc.tensor.matmul(
-                        d_everywhere[:, 0:rows, 2 * a : 2 * a + 2, :], side[a][:], lone[:, 0:rows], start=True, stop=True
-                    )
-                gap = stream.tile([K, PAIR, Q, A], F32, name="gap")
-                nc.vector.tensor_scalar_add(gap[:, 0:rows], d_everywhere[:, 0:rows], minus_center[:])
-                gap2 = stream.tile([K, PAIR, Q, A], F32, name="gap2")
-                nc.vector.tensor_tensor(gap2[:, 0:rows], gap[:, 0:rows], gap[:, 0:rows], ALU.mult)
-                nc.scalar.activation(rbf[:, s0 : s0 + rows], gap2[:, 0:rows], ACT.Exp, scale=-GAMMA)
+                bracket = spread.tile([K, PAIR, Q, A], F32, name="bracket")
+                nc.tensor.matmul(bracket[:, 0:rows], spread_w[:], lone[:, 0:rows], start=True, stop=True)
+                nc.scalar.activation(
+                    rbf[:, s0 : s0 + rows],
+                    bracket[:, 0:rows],
+                    ACT.Exp,
+                    bias=minus_gamma_center2[:],
+                    scale=2.0 * GAMMA,
+                )
                 exponentials(0, 0, gate, [(s0, rows)])
 
         with (

@@ -7,7 +7,6 @@ I32 = mybir.dt.int32
 U16 = mybir.dt.uint16
 ACT = mybir.ActivationFunctionType
 ALU = mybir.AluOpType
-AXIS = mybir.AxisListType
 
 P = 128
 C = 512
@@ -206,25 +205,25 @@ def tile_crystalencoder_b_kernel(
             def add_shifted(total, row, right, stop=False):
                 nc.tensor.matmul(total[:, :, right : right + A], identity[:], row, start=False, stop=stop)
 
-            def looked_up_times_gate0(cb, step, gate, turned, total):
+            def looked_up_times_gate0(cb, step, gate, turned, total, unshifted):
                 product = products.tile([P, CHUNK, Q, A], F32, name="product")
                 forward = [2 * step, 2 * step + 1]
                 backward = [2 * step + 1, 2 * step + 2]
                 partners = [turned[:, s % 2] if s > 0 else gate[:, 0] for s in forward] + [gate[:, s] for s in backward]
                 rights = forward + [A - s for s in backward]
+                rows = [unshifted[:] if rights[i] == 0 else product[:, i] for i in range(CHUNK)]
                 for i in range(CHUNK):
-                    nc.vector.tensor_tensor(product[:, i], tables[cb][:].indirect(offsets[:]), partners[i], ALU.mult)
+                    nc.vector.tensor_tensor(rows[i], tables[cb][:].indirect(offsets[:]), partners[i], ALU.mult)
                 for i in range(CHUNK):
-                    add_shifted(total, product[:, i], rights[i], stop=(backward[1] == HALF and i == CHUNK - 1))
+                    if rights[i] > 0:
+                        add_shifted(total, rows[i], rights[i], stop=(backward[1] == HALF and i == CHUNK - 1))
 
-            def round_to_agg(l, cb, total):
-                with nc.allow_low_precision(reason="the sum of two float32 values is rounded once, to agg's bfloat16"):
-                    nc.vector.tensor_reduce(
-                        agg[l][:, cb, :].rearrange("p (q r) -> p q r", q=Q),
-                        total[:].rearrange("p q (h r) -> p q r h", h=2),
-                        axis=AXIS.X,
-                        op=ALU.add,
-                    )
+            def round_to_agg(l, cb, total, unshifted):
+                partial = small.tile([P, Q, A], F32, name="partial", tag="result")
+                nc.vector.tensor_tensor(partial[:], total[:, :, 0:A], unshifted, ALU.add)
+                nc.vector.tensor_tensor(
+                    agg[l][:, cb, :].rearrange("p (q r) -> p q r", q=Q), total[:, :, A : 2 * A], partial[:], ALU.add
+                )
 
             def node_update(l, ob):
                 z = banks.tile([P, Q, A], F32, name="z", tag="pre")
@@ -245,7 +244,7 @@ def tile_crystalencoder_b_kernel(
             steps = HALF // 2
             one_at_last = one_after_exponentials(gate)
             turned = {}
-            cuts = [0, FIRST, THIRD, 2 * THIRD, SHIFTS]
+            cuts = [0, 1, 3, 5, 7, THIRD, 2 * THIRD, SHIFTS]
             for first_row, end_row in zip(cuts[:-1], cuts[1:]):
                 logarithm(gate, first_row, end_row, one_at_last)
                 for step in range(AHEAD):
@@ -255,18 +254,19 @@ def tile_crystalencoder_b_kernel(
                 l_next, cb_next = (0, cb + 1) if cb + 1 < CB else (1, 0)
                 upcoming = gates.tile([P, SHIFTS, Q, A], F32, name="upcoming", tag="gate")
                 total = empty_total()
+                unshifted = small.tile([P, Q, A], F32, name="unshifted", tag="result")
                 for step in range(steps):
                     later = step + AHEAD
                     if later < steps:
                         turned[(cb, later)] = turn(gate, later)
                     elif cb + 1 < CB:
                         turned[(cb + 1, later - steps)] = turn(upcoming, later - steps)
-                    looked_up_times_gate0(cb, step, gate, turned[(cb, step)], total)
+                    looked_up_times_gate0(cb, step, gate, turned[(cb, step)], total, unshifted)
                     some_banks = every_bank[4 * step : 4 * step + 4]
                     exponentials(l_next, cb_next, upcoming, some_banks)
                     if some_banks and some_banks[-1] == every_bank[-1]:
                         logarithms(upcoming)
-                round_to_agg(0, cb, total)
+                round_to_agg(0, cb, total, unshifted[:])
                 gate = upcoming
 
             for ob in range(CB):
@@ -315,11 +315,7 @@ def tile_crystalencoder_b_kernel(
                 folder = nc.vector if last_block else nc.gpsimd
                 folder.tensor_tensor(four_rows[:, 0:2], four_rows[:, 0:2], four_rows[:, 2:4], ALU.add)
                 folder.tensor_tensor(four_rows[:, 0], four_rows[:, 0], four_rows[:, 1], ALU.add)
-                partial = small.tile([P, Q, A], F32, name="partial", tag="result")
-                nc.vector.tensor_tensor(partial[:], total[:, :, 0:A], four_rows[:, 0], ALU.add)
-                nc.vector.tensor_tensor(
-                    agg[1][:, cb, :].rearrange("p (q r) -> p q r", q=Q), total[:, :, A : 2 * A], partial[:], ALU.add
-                )
+                round_to_agg(1, cb, total, four_rows[:, 0])
                 gate = upcoming
 
             for ob in range(CB):

@@ -1,3 +1,5 @@
+import math
+
 import concourse.mybir as mybir
 from concourse.masks import make_identity
 
@@ -22,6 +24,7 @@ VMAX = 8.0
 GAMMA = 1.0 / (VMAX / K) ** 2
 EPS = 1e-6
 STEP = VMAX / (K - 1)
+T_SELF = math.sqrt(EPS) - VMAX / 2
 MIDDLE = VMAX / 2
 HALF = A // 2
 SHIFTS = HALF + 1
@@ -145,9 +148,19 @@ def tile_crystalencoder_b_kernel(
             )
 
             gate = gates.tile([P, SHIFTS, Q, A], F32, name="gate", tag="gate")
+            self_bias = geometry.tile([K, 1], F32, name="self_bias")
+            nc.vector.tensor_scalar_add(self_bias[:], minus_gamma_center2[:], -GAMMA * T_SELF * T_SELF)
+            nc.scalar.activation(
+                rbf[:, 0],
+                center[:].unsqueeze(2).to_broadcast([K, Q, A]),
+                ACT.Exp,
+                bias=self_bias[:],
+                scale=2.0 * GAMMA * T_SELF,
+            )
             for s0, rows in banks_of_rows():
                 lone = stream.tile([P, PAIR, Q, A], F32, name="lone")
-                for i in range(rows):
+                made = range(1, rows) if s0 == 0 else range(rows)
+                for i in made:
                     first = HALF - (s0 + i)
                     nc.vector.tensor_tensor(
                         lone[:, i],
@@ -156,10 +169,10 @@ def tile_crystalencoder_b_kernel(
                         ALU.mult,
                     )
                 bracket = spread.tile([K, PAIR, Q, A], F32, name="bracket")
-                nc.tensor.matmul(bracket[:, 0:rows], spread_w[:], lone[:, 0:rows], start=True, stop=True)
+                nc.tensor.matmul(bracket[:, made[0] : rows], spread_w[:], lone[:, made[0] : rows], start=True, stop=True)
                 nc.scalar.activation(
-                    rbf[:, s0 : s0 + rows],
-                    bracket[:, 0:rows],
+                    rbf[:, s0 + made[0] : s0 + rows],
+                    bracket[:, made[0] : rows],
                     ACT.Exp,
                     bias=minus_gamma_center2[:],
                     scale=2.0 * GAMMA,

import math

import concourse.mybir as mybir
from concourse.masks import make_identity

F32 = mybir.dt.float32
BF16 = mybir.dt.bfloat16
I32 = mybir.dt.int32
U16 = mybir.dt.uint16
ACT = mybir.ActivationFunctionType
ALU = mybir.AluOpType

P = 128
C = 512
CB = C // P
S = 4096
K = 128
N = 256
A = 64
Q = N // A
XYZ = 3
BANK = 512
VMAX = 8.0
GAMMA = 1.0 / (VMAX / K) ** 2
EPS = 1e-6
STEP = VMAX / (K - 1)
T_SELF = math.sqrt(EPS) - VMAX / 2
MIDDLE = VMAX / 2
HALF = A // 2
SHIFTS = HALF + 1
PAIR = BANK // N
THIRD = SHIFTS // 3
FIRST = 3
CHUNK = 4
AHEAD = 11

FLOPS = 2 * (2 * K * C * A * N + 2 * C * C * N)


def banks_of_rows():
    return [(s, min(PAIR, SHIFTS - s)) for s in range(0, SHIFTS, PAIR)]


def tile_crystalencoder_b_kernel(
    tc, table, cart, edge_w0, edge_b0, node_w0, node_b0, edge_w1, edge_b1, node_w1, node_b1, offs, out
):
    nc = tc.nc
    with (
        tc.tile_pool(name="held", bufs=1) as held,
        tc.tile_pool(name="gates", bufs=2) as gates,
        tc.psum_pool(name="banks", bufs=4) as banks,
    ):
        offsets = held.tile([P, N // 16], U16, name="offsets")

        edge_w = [held.tile([K, C], BF16, name=f"edge_w{l}") for l in range(2)]
        node_w = [held.tile([P, CB, C], BF16, name=f"node_w{l}") for l in range(2)]
        edge_b = [held.tile([P, CB], F32, name=f"edge_b{l}") for l in range(2)]
        node_b = [held.tile([P, CB], F32, name=f"node_b{l}") for l in range(2)]
        tables = [held.tile([P, S], F32, name=f"table{cb}") for cb in range(CB)]
        rbf = held.tile([K, SHIFTS, Q, A], BF16, name="rbf")
        h1 = [held.tile([P, Q, A], F32, name=f"h1_{cb}") for cb in range(CB)]
        agg = [held.tile([P, CB, N], BF16, name=f"agg{l}") for l in range(2)]
        basis_index = held.tile([K, 1], I32, name="basis_index")
        nc.gpsimd.iota(basis_index[:], pattern=[[0, 1]], base=0, channel_multiplier=1)
        basis_along = held.tile([P, K], I32, name="basis_along")
        nc.gpsimd.iota(basis_along[:], pattern=[[1, K]], base=0, channel_multiplier=0)
        center = held.tile([K, 1], F32, name="center")
        nc.vector.tensor_scalar(center[:], basis_index[:], STEP, -MIDDLE, op0=ALU.mult, op1=ALU.add)
        minus_gamma_center2 = held.tile([K, 1], F32, name="minus_gamma_center2")
        nc.vector.scalar_tensor_tensor(
            minus_gamma_center2[:], center[:], -GAMMA, center[:], op0=ALU.mult, op1=ALU.mult
        )
        spread_w = held.tile([P, K], F32, name="spread_w")
        nc.vector.tensor_scalar(spread_w[0:A], basis_along[0:A], STEP, -MIDDLE, op0=ALU.mult, op1=ALU.add)
        nc.vector.memset(spread_w[A : 2 * A], -0.5)
        minus_middle = held.tile([P, 1], F32, name="minus_middle")
        nc.vector.memset(minus_middle[:], -MIDDLE)
        identity = held.tile([P, P], F32, name="identity")
        make_identity(nc, identity[:])

        zeros = held.tile([P, Q, 2 * A], BF16, name="zeros")
        nc.vector.memset(zeros[:], 0.0)
        identity_bf16 = held.tile([P, P], BF16, name="identity_bf16")
        make_identity(nc, identity_bf16[:])

        def exponentials(l, cb, gate, some_banks):
            for s0, rows in some_banks:
                pre = banks.tile([P, PAIR, Q, A], F32, name="pre")
                nc.tensor.matmul(
                    pre[:, 0:rows], edge_w[l][:, cb * P : (cb + 1) * P], rbf[:, s0 : s0 + rows], start=True, stop=True
                )
                nc.scalar.activation(
                    gate[:, s0 : s0 + rows], pre[:, 0:rows], ACT.Exp, bias=edge_b[l][:, cb : cb + 1]
                )

        with (
            tc.tile_pool(name="geometry", bufs=1) as geometry,
            tc.tile_pool(name="stream", bufs=3) as stream,
            tc.psum_pool(name="spread", bufs=2) as spread,
        ):
            cart_rows = geometry.tile([XYZ * Q, 2 * A], F32, name="cart_rows")
            for e in range(XYZ):
                nc.sync.dma_start(
                    cart_rows[e * Q : (e + 1) * Q].rearrange("p (u r) -> p u r", u=2),
                    cart[e].rearrange("(q r) -> q r", q=Q).unsqueeze(1).to_broadcast([Q, 2, A]),
                )
            atoms = geometry.tile([P, XYZ * N], F32, name="atoms")
            nc.sync.dma_start(atoms[:], cart.rearrange("e t -> (e t)").partition_broadcast(P))
            nc.sync.dma_start(offsets[:], offs)

            def load_bias(queue, tile, bias):
                with nc.allow_non_contiguous_dma(reason="one bias value to a partition"):
                    queue.dma_start(tile[:], bias.rearrange("(a p) o -> p (a o)", p=P))

            nc.sync.dma_start(edge_w[0][:], edge_w0)
            load_bias(nc.sync, edge_b[0], edge_b0)
            for cb in range(CB):
                nc.sync.dma_start(tables[cb][:], table[cb * P : (cb + 1) * P, :])
            nc.sync.dma_start(node_w[0][:], node_w0.rearrange("(m p) c -> p m c", p=P))
            load_bias(nc.sync, node_b[0], node_b0)
            nc.sync.dma_start(edge_w[1][:], edge_w1)
            load_bias(nc.sync, edge_b[1], edge_b1)
            nc.sync.dma_start(node_w[1][:], node_w1.rearrange("(m p) c -> p m c", p=P))
            load_bias(nc.sync, node_b[1], node_b1)

            is_atom = geometry.tile([P, A], F32, name="is_atom")
            nc.vector.tensor_tensor(is_atom[:], identity[:, 0:A], identity[:, A : 2 * A], ALU.add)
            own = banks.tile([P, XYZ * Q], F32, name="own", tag="pre")
            nc.tensor.matmul(own[:], cart_rows[:], identity[0 : XYZ * Q, 0 : XYZ * Q], start=True, stop=True)
            diff = geometry.tile([P, XYZ * Q, A], F32, name="diff")
            nc.vector.tensor_tensor(
                diff[:],
                atoms[:].rearrange("p (g j) -> p g j", j=A),
                own[:].unsqueeze(2).to_broadcast([P, XYZ * Q, A]),
                ALU.subtract,
            )
            nc.vector.tensor_tensor(diff[:], diff[:], diff[:], ALU.mult)
            dist2 = geometry.tile([P, Q, A], F32, name="dist2")
            nc.vector.tensor_tensor(dist2[:], diff[:, 0:Q], diff[:, Q : 2 * Q], ALU.add)
            nc.vector.scalar_tensor_tensor(dist2[:], dist2[:], EPS, diff[:, 2 * Q : 3 * Q], op0=ALU.add, op1=ALU.add)
            dist_around = geometry.tile([P, Q, HALF + A], F32, name="dist_around")
            nc.scalar.activation(dist_around[:, :, HALF : HALF + A], dist2[:], ACT.Sqrt)
            nc.scalar.activation(dist_around[:, :, 0:HALF], dist2[:, :, HALF:A], ACT.Sqrt)
            t_around = geometry.tile([P, Q, HALF + A], F32, name="t_around")
            nc.vector.tensor_scalar_add(t_around[0:A], dist_around[0:A], -MIDDLE)
            nc.scalar.activation(
                t_around[A : 2 * A], dist_around[A : 2 * A], ACT.Square, bias=minus_middle[A : 2 * A]
            )

            gate = gates.tile([P, SHIFTS, Q, A], F32, name="gate", tag="gate")
            self_bias = geometry.tile([K, 1], F32, name="self_bias")
            nc.vector.tensor_scalar_add(self_bias[:], minus_gamma_center2[:], -GAMMA * T_SELF * T_SELF)
            nc.scalar.activation(
                rbf[:, 0],
                center[:].unsqueeze(2).to_broadcast([K, Q, A]),
                ACT.Exp,
                bias=self_bias[:],
                scale=2.0 * GAMMA * T_SELF,
            )
            for s0, rows in banks_of_rows():
                lone = stream.tile([P, PAIR, Q, A], F32, name="lone")
                made = range(1, rows) if s0 == 0 else range(rows)
                for i in made:
                    first = HALF - (s0 + i)
                    nc.vector.tensor_tensor(
                        lone[:, i],
                        t_around[:, :, first : first + A],
                        is_atom[:].unsqueeze(1).to_broadcast([P, Q, A]),
                        ALU.mult,
                    )
                bracket = spread.tile([K, PAIR, Q, A], F32, name="bracket")
                nc.tensor.matmul(bracket[:, made[0] : rows], spread_w[:], lone[:, made[0] : rows], start=True, stop=True)
                nc.scalar.activation(
                    rbf[:, s0 + made[0] : s0 + rows],
                    bracket[:, made[0] : rows],
                    ACT.Exp,
                    bias=minus_gamma_center2[:],
                    scale=2.0 * GAMMA,
                )
                exponentials(0, 0, gate, [(s0, rows)])

        with (
            tc.tile_pool(name="products", bufs=9) as products,
            tc.tile_pool(name="turns", bufs=AHEAD + 2) as turns,
            tc.tile_pool(name="small", bufs=CB) as small,
            tc.psum_pool(name="sums", bufs=2) as sums,
            tc.psum_pool(name="around", bufs=2) as around,
        ):

            def one_after_exponentials(gate):
                one_at_last = small.tile([P, 1], F32, name="one_at_last")
                nc.scalar.activation(one_at_last[:], gate[:, SHIFTS - 1, Q - 1, A - 1 : A], ACT.Copy, bias=1.0, scale=0.0)
                return one_at_last

            def logarithm(gate, first_row, end_row, one_at_last):
                rows = gate[:, first_row:end_row]
                nc.scalar.activation(rows, rows, ACT.Ln, bias=one_at_last[:])

            def logarithms(gate):
                one_at_last = one_after_exponentials(gate)
                for first_row in range(0, SHIFTS, THIRD):
                    logarithm(gate, first_row, first_row + THIRD, one_at_last)

            def turn(gate, step):
                turned = turns.tile([P, 2, Q, A], F32, name="turned")
                for i in range(2):
                    s = 2 * step + i
                    if s > 0:
                        nc.scalar.copy(turned[:, i, :, 0 : A - s], gate[:, s, :, s:A])
                        nc.scalar.copy(turned[:, i, :, A - s : A], gate[:, s, :, 0:s])
                return turned

            def empty_total():
                total = sums.tile([P, Q, 2 * A], F32, name="total")
                nc.tensor.matmul(total[:], identity_bf16[:], zeros[:], start=True, stop=False)
                return total

            def add_shifted(total, row, right, stop=False):
                nc.tensor.matmul(total[:, :, right : right + A], identity[:], row, start=False, stop=stop)

            def looked_up_times_gate0(cb, step, gate, turned, total, unshifted):
                product = products.tile([P, CHUNK, Q, A], F32, name="product")
                forward = [2 * step, 2 * step + 1]
                backward = [2 * step + 1, 2 * step + 2]
                partners = [turned[:, s % 2] if s > 0 else gate[:, 0] for s in forward] + [gate[:, s] for s in backward]
                rights = forward + [A - s for s in backward]
                rows = [unshifted[:] if rights[i] == 0 else product[:, i] for i in range(CHUNK)]
                for i in range(CHUNK):
                    nc.vector.tensor_tensor(rows[i], tables[cb][:].indirect(offsets[:]), partners[i], ALU.mult)
                for i in range(CHUNK):
                    if rights[i] > 0:
                        add_shifted(total, rows[i], rights[i], stop=(backward[1] == HALF and i == CHUNK - 1))

            def round_to_agg(l, cb, total, unshifted):
                partial = small.tile([P, Q, A], F32, name="partial", tag="result")
                nc.vector.tensor_tensor(partial[:], total[:, :, 0:A], unshifted, ALU.add)
                nc.vector.tensor_tensor(
                    agg[l][:, cb, :].rearrange("p (q r) -> p q r", q=Q), total[:, :, A : 2 * A], partial[:], ALU.add
                )

            def node_update(l, ob):
                z = banks.tile([P, Q, A], F32, name="z", tag="pre")
                for mb in range(CB):
                    nc.tensor.matmul(
                        z[:].rearrange("p q r -> p (q r)"),
                        node_w[l][:, mb, ob * P : (ob + 1) * P],
                        agg[l][:, mb, :],
                        start=(mb == 0),
                        stop=(mb == CB - 1),
                    )
                update = small.tile([P, Q, A], F32, name="update")
                nc.scalar.activation(update[:], z[:], ACT.Silu, bias=node_b[l][:, ob : ob + 1])
                return update

            every_bank = banks_of_rows()

            steps = HALF // 2
            one_at_last = one_after_exponentials(gate)
            turned = {}
            cuts = [0, 1, 3, 5, 7, THIRD, 2 * THIRD, SHIFTS]
            for first_row, end_row in zip(cuts[:-1], cuts[1:]):
                logarithm(gate, first_row, end_row, one_at_last)
                for step in range(AHEAD):
                    if first_row <= 2 * step + 1 < end_row:
                        turned[(0, step)] = turn(gate, step)
            for cb in range(CB):
                l_next, cb_next = (0, cb + 1) if cb + 1 < CB else (1, 0)
                upcoming = gates.tile([P, SHIFTS, Q, A], F32, name="upcoming", tag="gate")
                total = empty_total()
                unshifted = small.tile([P, Q, A], F32, name="unshifted", tag="result")
                for step in range(steps):
                    later = step + AHEAD
                    if later < steps:
                        turned[(cb, later)] = turn(gate, later)
                    elif cb + 1 < CB:
                        turned[(cb + 1, later - steps)] = turn(upcoming, later - steps)
                    looked_up_times_gate0(cb, step, gate, turned[(cb, step)], total, unshifted)
                    some_banks = every_bank[4 * step : 4 * step + 4]
                    exponentials(l_next, cb_next, upcoming, some_banks)
                    if some_banks and some_banks[-1] == every_bank[-1]:
                        logarithms(upcoming)
                round_to_agg(0, cb, total, unshifted[:])
                gate = upcoming

            for ob in range(CB):
                update = node_update(0, ob)
                for piece in range(2):
                    crystals = slice(piece * (Q // 2), (piece + 1) * (Q // 2))
                    nc.vector.tensor_tensor(
                        h1[ob][:, crystals],
                        tables[ob][:].indirect(offsets[:, piece * (N // 32) : (piece + 1) * (N // 32)]),
                        update[:, crystals],
                        ALU.add,
                    )

            steps = HALF // CHUNK
            for cb in range(CB):
                last_block = cb == CB - 1
                if cb + 1 < CB:
                    upcoming = gates.tile([P, SHIFTS, Q, A], F32, name="upcoming", tag="gate")
                h1_around = around.tile([P, Q, HALF + A], F32, name="h1_around")
                nc.tensor.matmul(h1_around[:, :, 0:HALF], identity[:], h1[cb][:, :, HALF:A], start=True, stop=True)
                nc.tensor.matmul(h1_around[:, :, HALF : HALF + A], identity[:], h1[cb][:], start=True, stop=True)
                total = empty_total()
                if cb + 1 < CB:
                    exponentials(1, cb + 1, upcoming, every_bank)
                    logarithms(upcoming)
                for step in range(steps):
                    forward = products.tile([P, CHUNK, Q, A], F32, name="forward", tag="product")
                    backward = products.tile([P, CHUNK, Q, A], F32, name="backward", tag="product")
                    for i in range(CHUNK):
                        s = CHUNK * step + i
                        nc.vector.tensor_tensor(forward[:, i], gate[:, s], h1_around[:, :, HALF - s : HALF - s + A], ALU.mult)
                    s0 = CHUNK * step + 1
                    nc.vector.tensor_tensor(
                        backward[:],
                        gate[:, s0 : s0 + CHUNK],
                        h1_around[:, :, HALF : HALF + A].unsqueeze(1).to_broadcast([P, CHUNK, Q, A]),
                        ALU.mult,
                    )
                    for i in range(CHUNK):
                        add_shifted(total, backward[:, i], A - (s0 + i), stop=(s0 + i == HALF))
                    if step == 0:
                        four_rows = forward
                    else:
                        adder = nc.vector if last_block and step == steps - 1 else nc.gpsimd
                        adder.tensor_tensor(four_rows[:], four_rows[:], forward[:], ALU.add)
                folder = nc.vector if last_block else nc.gpsimd
                folder.tensor_tensor(four_rows[:, 0:2], four_rows[:, 0:2], four_rows[:, 2:4], ALU.add)
                folder.tensor_tensor(four_rows[:, 0], four_rows[:, 0], four_rows[:, 1], ALU.add)
                round_to_agg(1, cb, total, four_rows[:, 0])
                gate = upcoming

            for ob in range(CB):
                update = node_update(1, ob)
                result = small.tile([P, Q, A], F32, name="result")
                nc.vector.tensor_tensor(result[:], h1[ob][:], update[:], ALU.add)
                nc.sync.dma_start(out[ob * P : (ob + 1) * P, :], result[:].rearrange("p q r -> p (q r)"))
